import numpy as np
import ml_dtypes


def mxq(x, axis, fmt="e4m3"):
    dtype, down = {"e4m3": (ml_dtypes.float8_e4m3fn, 7), "e5m2": (ml_dtypes.float8_e5m2, 14)}[fmt]
    v = np.moveaxis(np.asarray(x, np.float32).astype(ml_dtypes.bfloat16).astype(np.float64), axis, -1)
    blocks = v.reshape(v.shape[:-1] + (-1, 32))
    amax = np.abs(blocks).max(-1, keepdims=True)
    byte = np.maximum(np.where(amax > 0, np.frexp(amax)[1] - 1 + 127, 0) - down, 1)
    scale = np.exp2(byte - 127.0)
    codes = (blocks / scale).astype(np.float32).astype(dtype).astype(np.float64)
    return np.moveaxis((codes * scale).reshape(v.shape), -1, axis)


WIDE = False


def mx_kscale(k):
    if not WIDE:
        return np.ones(k)
    levels = np.array([10, -10, 5, -5, 0])
    a = np.random.permutation(np.resize(levels, k // 512 * 4)).reshape(k // 512, 4)
    idx = np.arange(k)
    return np.exp2(a[idx // 512, idx % 128 // 32])


BF16 = ml_dtypes.bfloat16


def bf(x):
    return np.asarray(x, np.float32).astype(BF16)


def f64(x):
    return np.asarray(x).astype(np.float64)


B, C, H, W, HS, WS = 4, 1024, 16, 16, 16, 32
N = H * W
EPS = 1e-5


def mean_variance_norm(flat):
    mu = flat.mean(axis=-1, keepdims=True)
    sd = np.sqrt(flat.var(axis=-1, ddof=1, keepdims=True) + EPS)
    return (flat - mu) / sd


def setup_inputs():
    s = mx_kscale(C)
    gain = 0.7 + 0.6 * np.random.random_sample((B, C, 1, 1))
    shift = 0.4 * np.random.standard_normal((B, C, 1, 1))
    return {"content": bf(np.random.standard_normal((B, C, H, W)) * gain + shift),
            "mean": bf(np.random.standard_normal((B, C, H, W)) * 0.3 * s[:, None, None]),
            "std": bf(np.abs(1.0 + 0.25 * np.random.standard_normal((B, C, H, W))) * s[:, None, None]),
            "out_w": bf(np.random.standard_normal((C, C)) / np.sqrt(C) / s),
            "out_b": bf(np.random.standard_normal(C) * 0.2)}


def reference(content, mean, std, out_w, out_b):
    x = f64(content).reshape(B, C, N)
    o = f64(std).reshape(B, C, N) * mean_variance_norm(x) + f64(mean).reshape(B, C, N)
    y = (mxq(f64(out_w), 1, "e4m3") @ mxq(o, 1, "e4m3")) + f64(out_b)[:, None]
    return (y + x).reshape(B, C, H, W)

@@ -1,0 +1,254 @@
+from contextlib import ExitStack
+
+import concourse.mybir as mybir
+from concourse.masks import make_identity
+
+F32 = mybir.dt.float32
+BF16 = mybir.dt.bfloat16
+U32 = mybir.dt.uint32
+U8 = mybir.dt.uint8
+FP8X4 = mybir.dt.float8_e4m3fn_x4
+ALU = mybir.AluOpType
+ACT = mybir.ActivationFunctionType
+
+B = 4
+C = 1024
+N = 256
+P = 128
+G = 2
+J = 4
+UNITS = B * G
+EPS = 1e-5
+FLOPS = 2 * C * C * B * N
+
+VECTOR_STATS = (0, 2, 4)
+E_LAG = 4
+WQ_STEP = (3, 5)
+
+
+def tile_aattn_pb_kernel(tc, content, mean, std, out_w, out_b, out):
+    nc = tc.nc
+    x_dram = content.rearrange("b (g p j) h w -> b p g (j h w)", g=G, p=P, j=J)
+    m_dram = mean.rearrange("b (g p j) h w -> b p g (j h w)", g=G, p=P, j=J)
+    s_dram = std.rearrange("b (g p j) h w -> b p g (j h w)", g=G, p=P, j=J)
+    o_dram = out.rearrange("b (g p j) h w -> b p g (j h w)", g=G, p=P, j=J)
+    w_dram = out_w.rearrange("(g p h j) k -> g h p j k", g=G, p=P, h=2, j=2)
+    b_dram = out_b.rearrange("(g p j) -> p g j", g=G, p=P, j=J)
+
+    with ExitStack() as ctx:
+        res = ctx.enter_context(tc.tile_pool(name="res", bufs=1))
+        work = ctx.enter_context(tc.tile_pool(name="work", bufs=3))
+        psw = ctx.enter_context(tc.psum_pool(name="psw", bufs=2))
+        psy = ctx.enter_context(tc.psum_pool(name="psy", bufs=4))
+        ctx.enter_context(tc.manual_schedule())
+
+        x_sb = [res.tile([P, G * J, N], BF16, name="x%d" % b) for b in range(B)]
+        s_sb = [res.tile([P, G * J, N], BF16, name="s%d" % b) for b in range(B)]
+        m_sb = [res.tile([P, G * J, N], BF16, name="m%d" % b) for b in range(B)]
+        w_sb = [res.tile([P, 2, C], BF16, name="w%d" % q) for q in range(4)]
+        bias_bf = res.tile([P, G, J], BF16, name="bias_bf")
+        bias = res.tile([P, G * J], F32, name="bias")
+
+        def load(dst, src):
+            nc.sync.dma_start(out=dst[:].rearrange("p (g j) n -> p g (j n)", g=G), in_=src)
+
+        def load_w(q):
+            nc.sync.dma_start(out=w_sb[q][:], in_=w_dram[q // 2, q % 2])
+
+        load(x_sb[0], x_dram[0])
+        load(s_sb[0], s_dram[0])
+        load(m_sb[0], m_dram[0])
+        load(x_sb[1], x_dram[1])
+        load_w(0)
+        load(s_sb[1], s_dram[1])
+        load_w(1)
+        load(m_sb[1], m_dram[1])
+        load(x_sb[2], x_dram[2])
+        load_w(2)
+        load(s_sb[2], s_dram[2])
+        load_w(3)
+        nc.sync.dma_start(out=bias_bf[:], in_=b_dram)
+        load(m_sb[2], m_dram[2])
+        load(x_sb[3], x_dram[3])
+        load(s_sb[3], s_dram[3])
+        load(m_sb[3], m_dram[3])
+
+        ident = res.tile([P, P], F32, name="ident")
+        make_identity(nc, ident[:])
+        eps_t = res.tile([P, 1], F32, name="eps_t")
+        nc.vector.memset(eps_t[:], EPS)
+        warm = res.tile([P, 1], F32, name="warm")
+        nc.scalar.activation(out=warm[:], in_=eps_t[:], func=ACT.Sqrt)
+
+        wg = res.tile([P, G, G * J, 4 * P], BF16, name="wg", align_bytes=64)
+        wgf = wg[:].bitcast(F32)
+        wc = res.tile([P, G, C], U32, name="wc", align_bytes=64)
+        ws = res.tile([P, G, C], U8, name="ws", align_bytes=64)
+        junk = res.tile([P, N], BF16, name="junk")
+        oc = [res.tile([P, G, N], U32, name="oc%d" % b, align_bytes=64) for b in range(B)]
+        osc = [res.tile([P, G, N], U8, name="osc%d" % b, align_bytes=64) for b in range(B)]
+        bst = [res.tile([P, J, 6], F32, name="bst%d" % u) for u in range(UNITS)]
+        mv = [res.tile([P, J, 2], F32, name="mv%d" % u) for u in range(UNITS)]
+        ssum = [res.tile([P, J], F32, name="ssum%d" % u) for u in range(UNITS)]
+        negmu = [res.tile([P, J], F32, name="negmu%d" % u) for u in range(UNITS)]
+        ssq = [res.tile([P, J], F32, name="ssq%d" % u) for u in range(UNITS)]
+        sd = [res.tile([P, J], F32, name="sd%d" % u) for u in range(UNITS)]
+        rstd = [res.tile([P, J], F32, name="rstd%d" % u) for u in range(UNITS)]
+        t_of = {}
+        o_of = {}
+        og_of = {}
+        py_of = {}
+
+        def rows(tiles, u, j):
+            return tiles[u // G][:, (u % G) * J + j, :]
+
+        def w_transpose_copy(mt):
+            wf = w_sb[mt // 2][:].bitcast(F32)
+            pw = psw.tile([P, G, 2, P], F32, name="pw")
+            for c in range(G):
+                for e in range(2):
+                    nc.tensor.transpose(
+                        out=pw[:, c, e, :],
+                        in_=wf[:, mt % 2, 256 * c + e : 256 * (c + 1) : 2],
+                        identity=ident[:],
+                    )
+            nc.scalar.copy(
+                out=wgf[:, :, mt, :].rearrange("p c (m e) -> p c m e", e=2),
+                in_=pw[:].rearrange("p c e m -> p c m e"),
+            )
+
+        def w_quantise(g):
+            for c in range(G):
+                nc.vector.quantize_mx(
+                    out=wc[:, c, 512 * g : 512 * (g + 1)].bitcast(FP8X4),
+                    scales=ws[:, c, 512 * g : 512 * (g + 1)],
+                    in_=wg[:, c, J * g : J * (g + 1), :].rearrange("p a k -> p (a k)"),
+                )
+
+        def vector_stats(u):
+            for j in range(J):
+                nc.vector.bn_stats(out=bst[u][:, j, :], in_=rows(x_sb, u, j))
+                nc.vector.bn_aggr(out=mv[u][:, j, :], in_=bst[u][:, j, :])
+
+        def scalar_first_moment(u):
+            for j in range(J):
+                nc.scalar.activation(
+                    out=junk[:], in_=rows(x_sb, u, j), func=ACT.Identity,
+                    accum_out=ssum[u][:, j : j + 1],
+                )
+            nc.scalar.mul(out=negmu[u][:], in_=ssum[u][:], mul=-1.0 / N)
+
+        def scalar_second_moment(u):
+            if u in VECTOR_STATS:
+                nc.scalar.activation(
+                    out=sd[u][:], in_=mv[u][:, :, 1], func=ACT.Sqrt,
+                    bias=eps_t[:], scale=float(N) / (N - 1),
+                )
+                return
+            for j in range(J):
+                nc.scalar.activation(
+                    out=junk[:], in_=rows(x_sb, u, j), func=ACT.Square,
+                    bias=negmu[u][:, j : j + 1], accum_out=ssq[u][:, j : j + 1],
+                )
+            nc.scalar.activation(
+                out=sd[u][:], in_=ssq[u][:], func=ACT.Sqrt,
+                bias=eps_t[:], scale=1.0 / (N - 1),
+            )
+
+        def centre_times_std(u):
+            t = work.tile([P, J, N], F32, name="t", bufs=2)
+            t_of[u] = t
+            for j in range(J):
+                if u in VECTOR_STATS:
+                    nc.vector.scalar_tensor_tensor(
+                        out=t[:, j, :], in0=rows(x_sb, u, j), scalar=mv[u][:, j, 0:1],
+                        in1=rows(s_sb, u, j), op0=ALU.subtract, op1=ALU.mult,
+                    )
+                else:
+                    nc.vector.scalar_tensor_tensor(
+                        out=t[:, j, :], in0=rows(x_sb, u, j), scalar=negmu[u][:, j : j + 1],
+                        in1=rows(s_sb, u, j), op0=ALU.add, op1=ALU.mult,
+                    )
+
+        def scale_plus_mean(u):
+            o = work.tile([P, J, N], BF16, name="o")
+            o_of[u] = o
+            nc.vector.reciprocal(out=rstd[u][:], in_=sd[u][:])
+            for j in range(J):
+                nc.vector.scalar_tensor_tensor(
+                    out=o[:, j, :], in0=t_of[u][:, j, :], scalar=rstd[u][:, j : j + 1],
+                    in1=rows(m_sb, u, j), op0=ALU.mult, op1=ALU.add,
+                )
+
+        def regroup(u):
+            og = work.tile([P, N, J], BF16, name="og", align_bytes=64)
+            og_of[u] = og
+            nc.scalar.copy(
+                out=og[:].rearrange("p (c i) t -> p c t i", i=4),
+                in_=o_of[u][:].rearrange("p t (c i) -> p c t i", i=4),
+            )
+
+        def quantise(u):
+            nc.vector.quantize_mx(
+                out=oc[u // G][:, u % G, :].bitcast(FP8X4),
+                scales=osc[u // G][:, u % G, :],
+                in_=og_of[u][:].rearrange("p w t -> p (w t)"),
+            )
+
+        def project(u):
+            b = u // G
+            py_of[u] = []
+            for a in range(J // 2):
+                py = psy.tile([P, 2, N], F32, name="py")
+                py_of[u].append(py)
+                for h in range(2):
+                    mt = (u % G) * J + 2 * a + h
+                    for c in range(G):
+                        nc.tensor.matmul_mx(
+                            out=py[:, h, :],
+                            lhsT=wc[:, c, P * mt : P * (mt + 1)].bitcast(FP8X4),
+                            lhsT_scale=ws[:, c, P * mt : P * (mt + 1)],
+                            rhs=oc[b][:, c, :].bitcast(FP8X4),
+                            rhs_scale=osc[b][:, c, :],
+                            start=(c == 0),
+                            stop=(c == G - 1),
+                        )
+
+        def finish(u):
+            ot = work.tile([P, J, N], F32, name="ot")
+            for j in range(J):
+                mt = (u % G) * J + j
+                nc.vector.scalar_tensor_tensor(
+                    out=ot[:, j, :], in0=py_of[u][j // 2][:, j % 2, :], scalar=bias[:, mt : mt + 1],
+                    in1=rows(x_sb, u, j), op0=ALU.add, op1=ALU.add,
+                )
+            nc.sync.dma_start(out=o_dram[u // G][:, u % G, :], in_=ot[:].rearrange("p j n -> p (j n)"))
+
+        vector_stats(0)
+        for i in range(UNITS + E_LAG):
+            if 1 <= i <= UNITS:
+                regroup(i - 1)
+            if i < UNITS:
+                scalar_second_moment(i)
+            if i + 1 < UNITS and (i + 1) not in VECTOR_STATS:
+                scalar_first_moment(i + 1)
+            if 1 <= i <= 4:
+                w_transpose_copy(2 * (i - 1))
+                w_transpose_copy(2 * (i - 1) + 1)
+
+            if i < UNITS:
+                centre_times_std(i)
+            if (i + 1) in VECTOR_STATS:
+                vector_stats(i + 1)
+            if 1 <= i <= UNITS:
+                quantise(i - 1)
+            if i in WQ_STEP:
+                w_quantise(WQ_STEP.index(i))
+            if i == E_LAG:
+                nc.vector.tensor_copy(out=bias[:], in_=bias_bf[:].rearrange("p g j -> p (g j)"))
+            if i >= E_LAG:
+                project(i - E_LAG)
+            if i < UNITS:
+                scale_plus_mean(i)
+            if i >= E_LAG:
+                finish(i - E_LAG)

@@ -22,8 +22,8 @@ EPS = 1e-5
 FLOPS = 2 * C * C * B * N
 
 VECTOR_STATS = (0, 2, 4)
-E_LAG = 4
-WQ_STEP = (3, 5)
+E_LAG = 5
+WQ_STEP = (2, 4)
 
 
 def tile_aattn_pb_kernel(tc, content, mean, std, out_w, out_b, out):
@@ -57,8 +57,8 @@ def tile_aattn_pb_kernel(tc, content, mean, std, out_w, out_b, out):
 
         load(x_sb[0], x_dram[0])
         load(s_sb[0], s_dram[0])
-        load(m_sb[0], m_dram[0])
         load(x_sb[1], x_dram[1])
+        load(m_sb[0], m_dram[0])
         load_w(0)
         load(s_sb[1], s_dram[1])
         load_w(1)
@@ -84,7 +84,7 @@ def tile_aattn_pb_kernel(tc, content, mean, std, out_w, out_b, out):
         wgf = wg[:].bitcast(F32)
         wc = res.tile([P, G, C], U32, name="wc", align_bytes=64)
         ws = res.tile([P, G, C], U8, name="ws", align_bytes=64)
-        junk = res.tile([P, N], BF16, name="junk")
+        junk = res.tile([P, 2 * J, N], BF16, name="junk")
         oc = [res.tile([P, G, N], U32, name="oc%d" % b, align_bytes=64) for b in range(B)]
         osc = [res.tile([P, G, N], U8, name="osc%d" % b, align_bytes=64) for b in range(B)]
         bst = [res.tile([P, J, 6], F32, name="bst%d" % u) for u in range(UNITS)]
@@ -125,35 +125,45 @@ def tile_aattn_pb_kernel(tc, content, mean, std, out_w, out_b, out):
                     in_=wg[:, c, J * g : J * (g + 1), :].rearrange("p a k -> p (a k)"),
                 )
 
-        def vector_stats(u):
+        def vector_partial_stats(u):
             for j in range(J):
                 nc.vector.bn_stats(out=bst[u][:, j, :], in_=rows(x_sb, u, j))
+
+        def vector_join_stats(u):
+            for j in range(J):
                 nc.vector.bn_aggr(out=mv[u][:, j, :], in_=bst[u][:, j, :])
 
-        def scalar_first_moment(u):
+        def scalar_sum(u):
             for j in range(J):
                 nc.scalar.activation(
-                    out=junk[:], in_=rows(x_sb, u, j), func=ACT.Identity,
+                    out=junk[:, j, :], in_=rows(x_sb, u, j), func=ACT.Identity,
                     accum_out=ssum[u][:, j : j + 1],
                 )
+
+        def scalar_negative_mean(u):
             nc.scalar.mul(out=negmu[u][:], in_=ssum[u][:], mul=-1.0 / N)
 
-        def scalar_second_moment(u):
+        def scalar_sum_of_squares(u):
+            for j in range(J):
+                nc.scalar.activation(
+                    out=junk[:, J + j, :], in_=rows(x_sb, u, j), func=ACT.Square,
+                    bias=negmu[u][:, j : j + 1], accum_out=ssq[u][:, j : j + 1],
+                )
+
+        def scalar_deviation(u):
             if u in VECTOR_STATS:
                 nc.scalar.activation(
                     out=sd[u][:], in_=mv[u][:, :, 1], func=ACT.Sqrt,
                     bias=eps_t[:], scale=float(N) / (N - 1),
                 )
-                return
-            for j in range(J):
+            else:
                 nc.scalar.activation(
-                    out=junk[:], in_=rows(x_sb, u, j), func=ACT.Square,
-                    bias=negmu[u][:, j : j + 1], accum_out=ssq[u][:, j : j + 1],
+                    out=sd[u][:], in_=ssq[u][:], func=ACT.Sqrt,
+                    bias=eps_t[:], scale=1.0 / (N - 1),
                 )
-            nc.scalar.activation(
-                out=sd[u][:], in_=ssq[u][:], func=ACT.Sqrt,
-                bias=eps_t[:], scale=1.0 / (N - 1),
-            )
+
+        def vector_reciprocal(u):
+            nc.vector.reciprocal(out=rstd[u][:], in_=sd[u][:])
 
         def centre_times_std(u):
             t = work.tile([P, J, N], F32, name="t", bufs=2)
@@ -173,7 +183,6 @@ def tile_aattn_pb_kernel(tc, content, mean, std, out_w, out_b, out):
         def scale_plus_mean(u):
             o = work.tile([P, J, N], BF16, name="o")
             o_of[u] = o
-            nc.vector.reciprocal(out=rstd[u][:], in_=sd[u][:])
             for j in range(J):
                 nc.vector.scalar_tensor_tensor(
                     out=o[:, j, :], in0=t_of[u][:, j, :], scalar=rstd[u][:, j : j + 1],
@@ -224,31 +233,44 @@ def tile_aattn_pb_kernel(tc, content, mean, std, out_w, out_b, out):
                 )
             nc.sync.dma_start(out=o_dram[u // G][:, u % G, :], in_=ot[:].rearrange("p j n -> p (j n)"))
 
-        vector_stats(0)
-        for i in range(UNITS + E_LAG):
-            if 1 <= i <= UNITS:
-                regroup(i - 1)
-            if i < UNITS:
-                scalar_second_moment(i)
-            if i + 1 < UNITS and (i + 1) not in VECTOR_STATS:
-                scalar_first_moment(i + 1)
-            if 1 <= i <= 4:
-                w_transpose_copy(2 * (i - 1))
-                w_transpose_copy(2 * (i - 1) + 1)
+        def on_vector(u):
+            return 0 <= u < UNITS and u in VECTOR_STATS
 
-            if i < UNITS:
+        def on_scalar(u):
+            return 0 <= u < UNITS and u not in VECTOR_STATS
+
+        def unit(u):
+            return 0 <= u < UNITS
+
+        for i in range(-3, UNITS + E_LAG):
+            if unit(i):
                 centre_times_std(i)
-            if (i + 1) in VECTOR_STATS:
-                vector_stats(i + 1)
-            if 1 <= i <= UNITS:
-                quantise(i - 1)
+                vector_reciprocal(i)
+            if on_vector(i + 1):
+                vector_join_stats(i + 1)
+            if unit(i - 2):
+                quantise(i - 2)
+            if on_vector(i + 2):
+                vector_partial_stats(i + 2)
+            if unit(i):
+                scale_plus_mean(i)
             if i in WQ_STEP:
                 w_quantise(WQ_STEP.index(i))
             if i == E_LAG:
                 nc.vector.tensor_copy(out=bias[:], in_=bias_bf[:].rearrange("p g j -> p (g j)"))
-            if i >= E_LAG:
+            if unit(i - E_LAG):
                 project(i - E_LAG)
-            if i < UNITS:
-                scale_plus_mean(i)
-            if i >= E_LAG:
                 finish(i - E_LAG)
+            if unit(i - 1):
+                regroup(i - 1)
+            if unit(i + 1):
+                scalar_deviation(i + 1)
+            if on_scalar(i + 2):
+                scalar_negative_mean(i + 2)
+            if on_scalar(i + 3):
+                scalar_sum(i + 3)
+            if 0 <= i < 4:
+                w_transpose_copy(2 * i)
+                w_transpose_copy(2 * i + 1)
+            if on_scalar(i + 2):
+                scalar_sum_of_squares(i + 2)

@@ -55,7 +55,10 @@ def tile_aattn_pb_kernel(tc, content, mean, std, out_w, out_b, out):
         def load_w(q):
             nc.sync.dma_start(out=w_sb[q][:], in_=w_dram[q // 2, q % 2])
 
-        load(x_sb[0], x_dram[0])
+        for g in range(G):
+            nc.sync.dma_start(
+                out=x_sb[0][:, g * J : (g + 1) * J, :].rearrange("p j n -> p (j n)"), in_=x_dram[0][:, g, :]
+            )
         load(s_sb[0], s_dram[0])
         load(x_sb[1], x_dram[1])
         load(m_sb[0], m_dram[0])
@@ -225,13 +228,31 @@ def tile_aattn_pb_kernel(tc, content, mean, std, out_w, out_b, out):
 
         def finish(u):
             ot = work.tile([P, J, N], F32, name="ot")
-            for j in range(J):
+            side = 0
+            yb = work.tile([P, N], F32, name="yb")
+            nc.scalar.activation(
+                out=yb[:], in_=py_of[u][side // 2][:, side % 2, :], func=ACT.Identity,
+                bias=bias[:, (u % G) * J + side : (u % G) * J + side + 1],
+            )
+            nc.gpsimd.tensor_tensor(out=ot[:, side, :], in0=yb[:], in1=rows(x_sb, u, side), op=ALU.add)
+            for j in range(1, J):
                 mt = (u % G) * J + j
                 nc.vector.scalar_tensor_tensor(
                     out=ot[:, j, :], in0=py_of[u][j // 2][:, j % 2, :], scalar=bias[:, mt : mt + 1],
                     in1=rows(x_sb, u, j), op0=ALU.add, op1=ALU.add,
                 )
-            nc.sync.dma_start(out=o_dram[u // G][:, u % G, :], in_=ot[:].rearrange("p j n -> p (j n)"))
+                if u == UNITS - 1 and j == 1:
+                    nc.sync.dma_start(
+                        out=o_dram[u // G][:, u % G, 0 : 2 * N],
+                        in_=ot[:, 0:2, :].rearrange("p j n -> p (j n)"),
+                    )
+            if u == UNITS - 1:
+                nc.sync.dma_start(
+                    out=o_dram[u // G][:, u % G, 2 * N : 4 * N],
+                    in_=ot[:, 2:4, :].rearrange("p j n -> p (j n)"),
+                )
+            else:
+                nc.sync.dma_start(out=o_dram[u // G][:, u % G, :], in_=ot[:].rearrange("p j n -> p (j n)"))
 
         def on_vector(u):
             return 0 <= u < UNITS and u in VECTOR_STATS

@@ -40,7 +40,6 @@ def tile_aattn_pb_kernel(tc, content, mean, std, out_w, out_b, out):
         work = ctx.enter_context(tc.tile_pool(name="work", bufs=3))
         psw = ctx.enter_context(tc.psum_pool(name="psw", bufs=2))
         psy = ctx.enter_context(tc.psum_pool(name="psy", bufs=4))
-        ctx.enter_context(tc.manual_schedule())
 
         x_sb = [res.tile([P, G * J, N], BF16, name="x%d" % b) for b in range(B)]
         s_sb = [res.tile([P, G * J, N], BF16, name="s%d" % b) for b in range(B)]
@@ -228,30 +227,18 @@ def tile_aattn_pb_kernel(tc, content, mean, std, out_w, out_b, out):
 
         def finish(u):
             ot = work.tile([P, J, N], F32, name="ot")
-            side = 0
-            yb = work.tile([P, N], F32, name="yb")
-            nc.scalar.activation(
-                out=yb[:], in_=py_of[u][side // 2][:, side % 2, :], func=ACT.Identity,
-                bias=bias[:, (u % G) * J + side : (u % G) * J + side + 1],
-            )
-            nc.gpsimd.tensor_tensor(out=ot[:, side, :], in0=yb[:], in1=rows(x_sb, u, side), op=ALU.add)
-            for j in range(1, J):
+            for j in range(J):
                 mt = (u % G) * J + j
                 nc.vector.scalar_tensor_tensor(
                     out=ot[:, j, :], in0=py_of[u][j // 2][:, j % 2, :], scalar=bias[:, mt : mt + 1],
                     in1=rows(x_sb, u, j), op0=ALU.add, op1=ALU.add,
                 )
-                if u == UNITS - 1 and j == 1:
+                if u == UNITS - 1 and j % 2 == 1:
                     nc.sync.dma_start(
-                        out=o_dram[u // G][:, u % G, 0 : 2 * N],
-                        in_=ot[:, 0:2, :].rearrange("p j n -> p (j n)"),
+                        out=o_dram[u // G][:, u % G, (j - 1) * N : (j + 1) * N],
+                        in_=ot[:, j - 1 : j + 1, :].rearrange("p j n -> p (j n)"),
                     )
-            if u == UNITS - 1:
-                nc.sync.dma_start(
-                    out=o_dram[u // G][:, u % G, 2 * N : 4 * N],
-                    in_=ot[:, 2:4, :].rearrange("p j n -> p (j n)"),
-                )
-            else:
+            if u < UNITS - 1:
                 nc.sync.dma_start(out=o_dram[u // G][:, u % G, :], in_=ot[:].rearrange("p j n -> p (j n)"))
 
         def on_vector(u):

@@ -227,18 +227,30 @@ def tile_aattn_pb_kernel(tc, content, mean, std, out_w, out_b, out):
 
         def finish(u):
             ot = work.tile([P, J, N], F32, name="ot")
-            for j in range(J):
+            side = 0
+            yb = work.tile([P, N], F32, name="yb")
+            nc.scalar.activation(
+                out=yb[:], in_=py_of[u][side // 2][:, side % 2, :], func=ACT.Identity,
+                bias=bias[:, (u % G) * J + side : (u % G) * J + side + 1],
+            )
+            nc.gpsimd.tensor_tensor(out=ot[:, side, :], in0=yb[:], in1=rows(x_sb, u, side), op=ALU.add)
+            for j in range(1, J):
                 mt = (u % G) * J + j
                 nc.vector.scalar_tensor_tensor(
                     out=ot[:, j, :], in0=py_of[u][j // 2][:, j % 2, :], scalar=bias[:, mt : mt + 1],
                     in1=rows(x_sb, u, j), op0=ALU.add, op1=ALU.add,
                 )
-                if u == UNITS - 1 and j % 2 == 1:
+                if u == UNITS - 1 and j == 1:
                     nc.sync.dma_start(
-                        out=o_dram[u // G][:, u % G, (j - 1) * N : (j + 1) * N],
-                        in_=ot[:, j - 1 : j + 1, :].rearrange("p j n -> p (j n)"),
+                        out=o_dram[u // G][:, u % G, 0 : 2 * N],
+                        in_=ot[:, 0:2, :].rearrange("p j n -> p (j n)"),
                     )
-            if u < UNITS - 1:
+            if u == UNITS - 1:
+                nc.sync.dma_start(
+                    out=o_dram[u // G][:, u % G, 2 * N : 4 * N],
+                    in_=ot[:, 2:4, :].rearrange("p j n -> p (j n)"),
+                )
+            else:
                 nc.sync.dma_start(out=o_dram[u // G][:, u % G, :], in_=ot[:].rearrange("p j n -> p (j n)"))
 
         def on_vector(u):

@@ -11,286 +11,283 @@ FP8X4 = mybir.dt.float8_e4m3fn_x4
 ALU = mybir.AluOpType
 ACT = mybir.ActivationFunctionType
 
-B = 4
-C = 1024
-N = 256
+IMAGES = 4
+CHANNELS = 1024
+PIXELS = 256
 P = 128
-G = 2
-J = 4
-UNITS = B * G
+HALVES = 2
+ROWS = 4
+HALF = ROWS * P
+PASS_WORDS = HALF // 2
+RUN = 4
+UNITS = IMAGES * HALVES
+TILES = HALVES * ROWS
 EPS = 1e-5
-FLOPS = 2 * C * C * B * N
+FLOPS = 2 * CHANNELS * CHANNELS * IMAGES * PIXELS
 
 VECTOR_STATS = (0, 2, 4)
-E_LAG = 5
-WQ_STEP = (2, 4)
+W_QUANTISE_STEPS = (2, 4)
+FINISH_LAG = 5
 
 
 def tile_aattn_pb_kernel(tc, content, mean, std, out_w, out_b, out):
     nc = tc.nc
-    x_dram = content.rearrange("b (g p j) h w -> b p g (j h w)", g=G, p=P, j=J)
-    m_dram = mean.rearrange("b (g p j) h w -> b p g (j h w)", g=G, p=P, j=J)
-    s_dram = std.rearrange("b (g p j) h w -> b p g (j h w)", g=G, p=P, j=J)
-    o_dram = out.rearrange("b (g p j) h w -> b p g (j h w)", g=G, p=P, j=J)
-    w_dram = out_w.rearrange("(g p h j) k -> g h p j k", g=G, p=P, h=2, j=2)
-    b_dram = out_b.rearrange("(g p j) -> p g j", g=G, p=P, j=J)
+    by_partition = "b (g p j) h w -> b p g (j h w)"
+    x_dram = content.rearrange(by_partition, g=HALVES, p=P, j=ROWS)
+    mean_dram = mean.rearrange(by_partition, g=HALVES, p=P, j=ROWS)
+    std_dram = std.rearrange(by_partition, g=HALVES, p=P, j=ROWS)
+    out_dram = out.rearrange(by_partition, g=HALVES, p=P, j=ROWS)
+    w_dram = out_w.rearrange("(g p h j) k -> g h p j k", g=HALVES, p=P, h=2, j=2)
+    bias_dram = out_b.rearrange("(g p j) -> p g j", g=HALVES, p=P, j=ROWS)
 
     with ExitStack() as ctx:
-        res = ctx.enter_context(tc.tile_pool(name="res", bufs=1))
+        keep = ctx.enter_context(tc.tile_pool(name="keep", bufs=1))
         work = ctx.enter_context(tc.tile_pool(name="work", bufs=3))
-        psw = ctx.enter_context(tc.psum_pool(name="psw", bufs=2))
-        psy = ctx.enter_context(tc.psum_pool(name="psy", bufs=4))
+        psum_w = ctx.enter_context(tc.psum_pool(name="psum_w", bufs=2))
+        psum_y = ctx.enter_context(tc.psum_pool(name="psum_y", bufs=4))
 
-        x_sb = [res.tile([P, G * J, N], BF16, name="x%d" % b) for b in range(B)]
-        s_sb = [res.tile([P, G * J, N], BF16, name="s%d" % b) for b in range(B)]
-        m_sb = [res.tile([P, G * J, N], BF16, name="m%d" % b) for b in range(B)]
-        w_sb = [res.tile([P, 2, C], BF16, name="w%d" % q) for q in range(4)]
-        bias_bf = res.tile([P, G, J], BF16, name="bias_bf")
-        bias = res.tile([P, G * J], F32, name="bias")
+        x_sb = [keep.tile([P, TILES, PIXELS], BF16, name="x%d" % b) for b in range(IMAGES)]
+        std_sb = [keep.tile([P, TILES, PIXELS], BF16, name="std%d" % b) for b in range(IMAGES)]
+        mean_sb = [keep.tile([P, TILES, PIXELS], BF16, name="mean%d" % b) for b in range(IMAGES)]
+        w_sb = [keep.tile([P, 2, CHANNELS], BF16, name="w%d" % q) for q in range(4)]
+        bias_bf = keep.tile([P, HALVES, ROWS], BF16, name="bias_bf")
 
-        def load(dst, src):
-            nc.sync.dma_start(out=dst[:].rearrange("p (g j) n -> p g (j n)", g=G), in_=src)
+        def load_content(b):
+            for g in range(HALVES):
+                nc.sync.dma_start(
+                    out=x_sb[b][:, g * ROWS : (g + 1) * ROWS, :].rearrange("p j n -> p (j n)"),
+                    in_=x_dram[b][:, g, :],
+                )
+
+        def load_image(tiles, dram, b):
+            nc.sync.dma_start(out=tiles[b][:].rearrange("p (g j) n -> p g (j n)", g=HALVES), in_=dram[b])
 
         def load_w(q):
             nc.sync.dma_start(out=w_sb[q][:], in_=w_dram[q // 2, q % 2])
 
-        for g in range(G):
-            nc.sync.dma_start(
-                out=x_sb[0][:, g * J : (g + 1) * J, :].rearrange("p j n -> p (j n)"), in_=x_dram[0][:, g, :]
-            )
-        load(s_sb[0], s_dram[0])
-        load(x_sb[1], x_dram[1])
-        load(m_sb[0], m_dram[0])
+        load_content(0)
+        load_image(std_sb, std_dram, 0)
+        load_content(1)
+        load_image(mean_sb, mean_dram, 0)
         load_w(0)
-        load(s_sb[1], s_dram[1])
+        load_image(std_sb, std_dram, 1)
         load_w(1)
-        load(m_sb[1], m_dram[1])
-        load(x_sb[2], x_dram[2])
+        load_image(mean_sb, mean_dram, 1)
+        load_content(2)
         load_w(2)
-        load(s_sb[2], s_dram[2])
+        load_image(std_sb, std_dram, 2)
         load_w(3)
-        nc.sync.dma_start(out=bias_bf[:], in_=b_dram)
-        load(m_sb[2], m_dram[2])
-        load(x_sb[3], x_dram[3])
-        load(s_sb[3], s_dram[3])
-        load(m_sb[3], m_dram[3])
+        nc.sync.dma_start(out=bias_bf[:], in_=bias_dram)
+        load_image(mean_sb, mean_dram, 2)
+        load_content(3)
+        load_image(std_sb, std_dram, 3)
+        load_image(mean_sb, mean_dram, 3)
 
-        ident = res.tile([P, P], F32, name="ident")
-        make_identity(nc, ident[:])
-        eps_t = res.tile([P, 1], F32, name="eps_t")
-        nc.vector.memset(eps_t[:], EPS)
-        warm = res.tile([P, 1], F32, name="warm")
-        nc.scalar.activation(out=warm[:], in_=eps_t[:], func=ACT.Sqrt)
+        identity = keep.tile([P, P], F32, name="identity")
+        make_identity(nc, identity[:])
+        eps = keep.tile([P, 1], F32, name="eps")
+        nc.vector.memset(eps[:], EPS)
+        first_sqrt = keep.tile([P, 1], F32, name="first_sqrt")
+        nc.scalar.activation(out=first_sqrt[:], in_=eps[:], func=ACT.Sqrt)
+        bias = keep.tile([P, TILES], F32, name="bias")
 
-        wg = res.tile([P, G, G * J, 4 * P], BF16, name="wg", align_bytes=64)
-        wgf = wg[:].bitcast(F32)
-        wc = res.tile([P, G, C], U32, name="wc", align_bytes=64)
-        ws = res.tile([P, G, C], U8, name="ws", align_bytes=64)
-        junk = res.tile([P, 2 * J, N], BF16, name="junk")
-        oc = [res.tile([P, G, N], U32, name="oc%d" % b, align_bytes=64) for b in range(B)]
-        osc = [res.tile([P, G, N], U8, name="osc%d" % b, align_bytes=64) for b in range(B)]
-        bst = [res.tile([P, J, 6], F32, name="bst%d" % u) for u in range(UNITS)]
-        mv = [res.tile([P, J, 2], F32, name="mv%d" % u) for u in range(UNITS)]
-        ssum = [res.tile([P, J], F32, name="ssum%d" % u) for u in range(UNITS)]
-        negmu = [res.tile([P, J], F32, name="negmu%d" % u) for u in range(UNITS)]
-        ssq = [res.tile([P, J], F32, name="ssq%d" % u) for u in range(UNITS)]
-        sd = [res.tile([P, J], F32, name="sd%d" % u) for u in range(UNITS)]
-        rstd = [res.tile([P, J], F32, name="rstd%d" % u) for u in range(UNITS)]
-        t_of = {}
-        o_of = {}
-        og_of = {}
-        py_of = {}
+        w_grouped = keep.tile([P, HALVES, TILES, ROWS * P], BF16, name="w_grouped", align_bytes=64)
+        w_words = keep.tile([P, HALVES, CHANNELS], U32, name="w_words", align_bytes=64)
+        w_scales = keep.tile([P, HALVES, CHANNELS], U8, name="w_scales", align_bytes=64)
+        o_words = [keep.tile([P, HALVES, PIXELS], U32, name="o_words%d" % b, align_bytes=64) for b in range(IMAGES)]
+        o_scales = [keep.tile([P, HALVES, PIXELS], U8, name="o_scales%d" % b, align_bytes=64) for b in range(IMAGES)]
 
-        def rows(tiles, u, j):
-            return tiles[u // G][:, (u % G) * J + j, :]
+        partial = {u: keep.tile([P, ROWS, 6], F32, name="partial%d" % u) for u in VECTOR_STATS}
+        mean_var = {u: keep.tile([P, ROWS, 2], F32, name="mean_var%d" % u) for u in VECTOR_STATS}
+        scalar_units = [u for u in range(UNITS) if u not in VECTOR_STATS]
+        total = {u: keep.tile([P, ROWS], F32, name="total%d" % u) for u in scalar_units}
+        minus_mu = {u: keep.tile([P, ROWS], F32, name="minus_mu%d" % u) for u in scalar_units}
+        squares = {u: keep.tile([P, ROWS], F32, name="squares%d" % u) for u in scalar_units}
+        deviation = [keep.tile([P, ROWS], F32, name="deviation%d" % u) for u in range(UNITS)]
+        inv_deviation = [keep.tile([P, ROWS], F32, name="inv_deviation%d" % u) for u in range(UNITS)]
+        unread = keep.tile([P, 2 * ROWS, PIXELS], BF16, name="unread")
 
-        def w_transpose_copy(mt):
-            wf = w_sb[mt // 2][:].bitcast(F32)
-            pw = psw.tile([P, G, 2, P], F32, name="pw")
-            for c in range(G):
+        centred = {}
+        modulated = {}
+        grouped = {}
+        projected = {}
+
+        def row(tiles, u, j):
+            return tiles[u // HALVES][:, (u % HALVES) * ROWS + j, :]
+
+        def w_transpose(tile_index):
+            words = w_sb[tile_index // 2][:].bitcast(F32)
+            planes = psum_w.tile([P, HALVES, 2, P], F32, name="planes")
+            for g in range(HALVES):
                 for e in range(2):
                     nc.tensor.transpose(
-                        out=pw[:, c, e, :],
-                        in_=wf[:, mt % 2, 256 * c + e : 256 * (c + 1) : 2],
-                        identity=ident[:],
+                        out=planes[:, g, e, :],
+                        in_=words[:, tile_index % 2, PASS_WORDS * g + e : PASS_WORDS * (g + 1) : 2],
+                        identity=identity[:],
                     )
             nc.scalar.copy(
-                out=wgf[:, :, mt, :].rearrange("p c (m e) -> p c m e", e=2),
-                in_=pw[:].rearrange("p c e m -> p c m e"),
+                out=w_grouped[:].bitcast(F32)[:, :, tile_index, :].rearrange("p g (m e) -> p g m e", e=2),
+                in_=planes[:].rearrange("p g e m -> p g m e"),
             )
 
-        def w_quantise(g):
-            for c in range(G):
+        def w_quantise(half):
+            for g in range(HALVES):
                 nc.vector.quantize_mx(
-                    out=wc[:, c, 512 * g : 512 * (g + 1)].bitcast(FP8X4),
-                    scales=ws[:, c, 512 * g : 512 * (g + 1)],
-                    in_=wg[:, c, J * g : J * (g + 1), :].rearrange("p a k -> p (a k)"),
+                    out=w_words[:, g, HALF * half : HALF * (half + 1)].bitcast(FP8X4),
+                    scales=w_scales[:, g, HALF * half : HALF * (half + 1)],
+                    in_=w_grouped[:, g, ROWS * half : ROWS * (half + 1), :].rearrange("p t k -> p (t k)"),
                 )
 
         def vector_partial_stats(u):
-            for j in range(J):
-                nc.vector.bn_stats(out=bst[u][:, j, :], in_=rows(x_sb, u, j))
+            for j in range(ROWS):
+                nc.vector.bn_stats(out=partial[u][:, j, :], in_=row(x_sb, u, j))
 
-        def vector_join_stats(u):
-            for j in range(J):
-                nc.vector.bn_aggr(out=mv[u][:, j, :], in_=bst[u][:, j, :])
+        def vector_mean_var(u):
+            for j in range(ROWS):
+                nc.vector.bn_aggr(out=mean_var[u][:, j, :], in_=partial[u][:, j, :])
 
-        def scalar_sum(u):
-            for j in range(J):
+        def scalar_total(u):
+            for j in range(ROWS):
                 nc.scalar.activation(
-                    out=junk[:, j, :], in_=rows(x_sb, u, j), func=ACT.Identity,
-                    accum_out=ssum[u][:, j : j + 1],
+                    out=unread[:, j, :], in_=row(x_sb, u, j), func=ACT.Identity,
+                    accum_out=total[u][:, j : j + 1],
                 )
 
-        def scalar_negative_mean(u):
-            nc.scalar.mul(out=negmu[u][:], in_=ssum[u][:], mul=-1.0 / N)
+        def scalar_minus_mu(u):
+            nc.scalar.mul(out=minus_mu[u][:], in_=total[u][:], mul=-1.0 / PIXELS)
 
-        def scalar_sum_of_squares(u):
-            for j in range(J):
+        def scalar_squares(u):
+            for j in range(ROWS):
                 nc.scalar.activation(
-                    out=junk[:, J + j, :], in_=rows(x_sb, u, j), func=ACT.Square,
-                    bias=negmu[u][:, j : j + 1], accum_out=ssq[u][:, j : j + 1],
+                    out=unread[:, ROWS + j, :], in_=row(x_sb, u, j), func=ACT.Square,
+                    bias=minus_mu[u][:, j : j + 1], accum_out=squares[u][:, j : j + 1],
                 )
 
         def scalar_deviation(u):
             if u in VECTOR_STATS:
                 nc.scalar.activation(
-                    out=sd[u][:], in_=mv[u][:, :, 1], func=ACT.Sqrt,
-                    bias=eps_t[:], scale=float(N) / (N - 1),
+                    out=deviation[u][:], in_=mean_var[u][:, :, 1], func=ACT.Sqrt,
+                    bias=eps[:], scale=float(PIXELS) / (PIXELS - 1),
                 )
             else:
                 nc.scalar.activation(
-                    out=sd[u][:], in_=ssq[u][:], func=ACT.Sqrt,
-                    bias=eps_t[:], scale=1.0 / (N - 1),
+                    out=deviation[u][:], in_=squares[u][:], func=ACT.Sqrt,
+                    bias=eps[:], scale=1.0 / (PIXELS - 1),
                 )
 
-        def vector_reciprocal(u):
-            nc.vector.reciprocal(out=rstd[u][:], in_=sd[u][:])
+        def vector_inverse(u):
+            nc.vector.reciprocal(out=inv_deviation[u][:], in_=deviation[u][:])
 
         def centre_times_std(u):
-            t = work.tile([P, J, N], F32, name="t", bufs=2)
-            t_of[u] = t
-            for j in range(J):
+            centred[u] = work.tile([P, ROWS, PIXELS], F32, name="centred", bufs=2)
+            for j in range(ROWS):
                 if u in VECTOR_STATS:
                     nc.vector.scalar_tensor_tensor(
-                        out=t[:, j, :], in0=rows(x_sb, u, j), scalar=mv[u][:, j, 0:1],
-                        in1=rows(s_sb, u, j), op0=ALU.subtract, op1=ALU.mult,
+                        out=centred[u][:, j, :], in0=row(x_sb, u, j), scalar=mean_var[u][:, j, 0:1],
+                        in1=row(std_sb, u, j), op0=ALU.subtract, op1=ALU.mult,
                     )
                 else:
                     nc.vector.scalar_tensor_tensor(
-                        out=t[:, j, :], in0=rows(x_sb, u, j), scalar=negmu[u][:, j : j + 1],
-                        in1=rows(s_sb, u, j), op0=ALU.add, op1=ALU.mult,
+                        out=centred[u][:, j, :], in0=row(x_sb, u, j), scalar=minus_mu[u][:, j : j + 1],
+                        in1=row(std_sb, u, j), op0=ALU.add, op1=ALU.mult,
                     )
 
         def scale_plus_mean(u):
-            o = work.tile([P, J, N], BF16, name="o")
-            o_of[u] = o
-            for j in range(J):
+            modulated[u] = work.tile([P, ROWS, PIXELS], BF16, name="modulated")
+            for j in range(ROWS):
                 nc.vector.scalar_tensor_tensor(
-                    out=o[:, j, :], in0=t_of[u][:, j, :], scalar=rstd[u][:, j : j + 1],
-                    in1=rows(m_sb, u, j), op0=ALU.mult, op1=ALU.add,
+                    out=modulated[u][:, j, :], in0=centred[u][:, j, :], scalar=inv_deviation[u][:, j : j + 1],
+                    in1=row(mean_sb, u, j), op0=ALU.mult, op1=ALU.add,
                 )
 
         def regroup(u):
-            og = work.tile([P, N, J], BF16, name="og", align_bytes=64)
-            og_of[u] = og
+            grouped[u] = work.tile([P, PIXELS, ROWS], BF16, name="grouped", align_bytes=64)
             nc.scalar.copy(
-                out=og[:].rearrange("p (c i) t -> p c t i", i=4),
-                in_=o_of[u][:].rearrange("p t (c i) -> p c t i", i=4),
+                out=grouped[u][:].rearrange("p (c i) j -> p c j i", i=RUN),
+                in_=modulated[u][:].rearrange("p j (c i) -> p c j i", i=RUN),
             )
 
         def quantise(u):
             nc.vector.quantize_mx(
-                out=oc[u // G][:, u % G, :].bitcast(FP8X4),
-                scales=osc[u // G][:, u % G, :],
-                in_=og_of[u][:].rearrange("p w t -> p (w t)"),
+                out=o_words[u // HALVES][:, u % HALVES, :].bitcast(FP8X4),
+                scales=o_scales[u // HALVES][:, u % HALVES, :],
+                in_=grouped[u][:].rearrange("p n j -> p (n j)"),
             )
 
         def project(u):
-            b = u // G
-            py_of[u] = []
-            for a in range(J // 2):
-                py = psy.tile([P, 2, N], F32, name="py")
-                py_of[u].append(py)
-                for h in range(2):
-                    mt = (u % G) * J + 2 * a + h
-                    for c in range(G):
+            b = u // HALVES
+            projected[u] = []
+            for pair in range(ROWS // 2):
+                bank = psum_y.tile([P, 2, PIXELS], F32, name="bank")
+                projected[u].append(bank)
+                for side in range(2):
+                    columns = slice(
+                        P * ((u % HALVES) * ROWS + 2 * pair + side), P * ((u % HALVES) * ROWS + 2 * pair + side + 1)
+                    )
+                    for g in range(HALVES):
                         nc.tensor.matmul_mx(
-                            out=py[:, h, :],
-                            lhsT=wc[:, c, P * mt : P * (mt + 1)].bitcast(FP8X4),
-                            lhsT_scale=ws[:, c, P * mt : P * (mt + 1)],
-                            rhs=oc[b][:, c, :].bitcast(FP8X4),
-                            rhs_scale=osc[b][:, c, :],
-                            start=(c == 0),
-                            stop=(c == G - 1),
+                            out=bank[:, side, :],
+                            lhsT=w_words[:, g, columns].bitcast(FP8X4),
+                            lhsT_scale=w_scales[:, g, columns],
+                            rhs=o_words[b][:, g, :].bitcast(FP8X4),
+                            rhs_scale=o_scales[b][:, g, :],
+                            start=(g == 0),
+                            stop=(g == HALVES - 1),
                         )
 
         def finish(u):
-            ot = work.tile([P, J, N], F32, name="ot")
-            side = 0
-            yb = work.tile([P, N], F32, name="yb")
-            nc.scalar.activation(
-                out=yb[:], in_=py_of[u][side // 2][:, side % 2, :], func=ACT.Identity,
-                bias=bias[:, (u % G) * J + side : (u % G) * J + side + 1],
-            )
-            nc.gpsimd.tensor_tensor(out=ot[:, side, :], in0=yb[:], in1=rows(x_sb, u, side), op=ALU.add)
-            for j in range(1, J):
-                mt = (u % G) * J + j
-                nc.vector.scalar_tensor_tensor(
-                    out=ot[:, j, :], in0=py_of[u][j // 2][:, j % 2, :], scalar=bias[:, mt : mt + 1],
-                    in1=rows(x_sb, u, j), op0=ALU.add, op1=ALU.add,
-                )
-                if u == UNITS - 1 and j == 1:
-                    nc.sync.dma_start(
-                        out=o_dram[u // G][:, u % G, 0 : 2 * N],
-                        in_=ot[:, 0:2, :].rearrange("p j n -> p (j n)"),
+            result = work.tile([P, ROWS, PIXELS], F32, name="result")
+            for pair in range(ROWS // 2):
+                for side in range(2):
+                    j = 2 * pair + side
+                    nc.vector.scalar_tensor_tensor(
+                        out=result[:, j, :], in0=projected[u][pair][:, side, :],
+                        scalar=bias[:, (u % HALVES) * ROWS + j : (u % HALVES) * ROWS + j + 1],
+                        in1=row(x_sb, u, j), op0=ALU.add, op1=ALU.add,
                     )
-            if u == UNITS - 1:
                 nc.sync.dma_start(
-                    out=o_dram[u // G][:, u % G, 2 * N : 4 * N],
-                    in_=ot[:, 2:4, :].rearrange("p j n -> p (j n)"),
+                    out=out_dram[u // HALVES][:, u % HALVES, 2 * pair * PIXELS : 2 * (pair + 1) * PIXELS],
+                    in_=result[:, 2 * pair : 2 * (pair + 1), :].rearrange("p j n -> p (j n)"),
                 )
-            else:
-                nc.sync.dma_start(out=o_dram[u // G][:, u % G, :], in_=ot[:].rearrange("p j n -> p (j n)"))
 
-        def on_vector(u):
-            return 0 <= u < UNITS and u in VECTOR_STATS
-
-        def on_scalar(u):
-            return 0 <= u < UNITS and u not in VECTOR_STATS
-
-        def unit(u):
+        def is_unit(u):
             return 0 <= u < UNITS
 
-        for i in range(-3, UNITS + E_LAG):
-            if unit(i):
+        def on_vector(u):
+            return is_unit(u) and u in VECTOR_STATS
+
+        def on_scalar(u):
+            return is_unit(u) and u not in VECTOR_STATS
+
+        for i in range(-3, UNITS + FINISH_LAG):
+            if is_unit(i):
                 centre_times_std(i)
-                vector_reciprocal(i)
+                vector_inverse(i)
             if on_vector(i + 1):
-                vector_join_stats(i + 1)
-            if unit(i - 2):
+                vector_mean_var(i + 1)
+            if is_unit(i - 2):
                 quantise(i - 2)
             if on_vector(i + 2):
                 vector_partial_stats(i + 2)
-            if unit(i):
+            if is_unit(i):
                 scale_plus_mean(i)
-            if i in WQ_STEP:
-                w_quantise(WQ_STEP.index(i))
-            if i == E_LAG:
+            if i in W_QUANTISE_STEPS:
+                w_quantise(W_QUANTISE_STEPS.index(i))
+            if i == FINISH_LAG:
                 nc.vector.tensor_copy(out=bias[:], in_=bias_bf[:].rearrange("p g j -> p (g j)"))
-            if unit(i - E_LAG):
-                project(i - E_LAG)
-                finish(i - E_LAG)
-            if unit(i - 1):
+            if is_unit(i - FINISH_LAG):
+                project(i - FINISH_LAG)
+                finish(i - FINISH_LAG)
+            if is_unit(i - 1):
                 regroup(i - 1)
-            if unit(i + 1):
+            if is_unit(i + 1):
                 scalar_deviation(i + 1)
             if on_scalar(i + 2):
-                scalar_negative_mean(i + 2)
+                scalar_minus_mu(i + 2)
             if on_scalar(i + 3):
-                scalar_sum(i + 3)
-            if 0 <= i < 4:
-                w_transpose_copy(2 * i)
-                w_transpose_copy(2 * i + 1)
+                scalar_total(i + 3)
+            if 0 <= 2 * i < TILES:
+                w_transpose(2 * i)
+                w_transpose(2 * i + 1)
             if on_scalar(i + 2):
-                scalar_sum_of_squares(i + 2)
+                scalar_squares(i + 2)

@@ -27,7 +27,7 @@ FLOPS = 2 * CHANNELS * CHANNELS * IMAGES * PIXELS
 
 VECTOR_STATS = (0, 2, 4)
 W_QUANTISE_STEPS = (2, 4)
-FINISH_LAG = 5
+FINISH_LAG = 4
 
 
 def tile_aattn_pb_kernel(tc, content, mean, std, out_w, out_b, out):

@@ -25,9 +25,10 @@ TILES = HALVES * ROWS
 EPS = 1e-5
 FLOPS = 2 * CHANNELS * CHANNELS * IMAGES * PIXELS
 
-VECTOR_STATS = (0, 2, 4)
+VECTOR_STATS = (0, 2, 4, 6)
 W_QUANTISE_STEPS = (2, 4)
 FINISH_LAG = 4
+TENSOR_UNITS = (2, 4, 6)
 
 
 def tile_aattn_pb_kernel(tc, content, mean, std, out_w, out_b, out):
@@ -45,6 +46,7 @@ def tile_aattn_pb_kernel(tc, content, mean, std, out_w, out_b, out):
         work = ctx.enter_context(tc.tile_pool(name="work", bufs=3))
         psum_w = ctx.enter_context(tc.psum_pool(name="psum_w", bufs=2))
         psum_y = ctx.enter_context(tc.psum_pool(name="psum_y", bufs=4))
+        psum_o = ctx.enter_context(tc.psum_pool(name="psum_o", bufs=2))
 
         x_sb = [keep.tile([P, TILES, PIXELS], BF16, name="x%d" % b) for b in range(IMAGES)]
         std_sb = [keep.tile([P, TILES, PIXELS], BF16, name="std%d" % b) for b in range(IMAGES)]
@@ -85,6 +87,8 @@ def tile_aattn_pb_kernel(tc, content, mean, std, out_w, out_b, out):
 
         identity = keep.tile([P, P], F32, name="identity")
         make_identity(nc, identity[:])
+        identity_bf = keep.tile([P, P], BF16, name="identity_bf")
+        make_identity(nc, identity_bf[:])
         eps = keep.tile([P, 1], F32, name="eps")
         nc.vector.memset(eps[:], EPS)
         first_sqrt = keep.tile([P, 1], F32, name="first_sqrt")
@@ -111,6 +115,7 @@ def tile_aattn_pb_kernel(tc, content, mean, std, out_w, out_b, out):
         modulated = {}
         grouped = {}
         projected = {}
+        summed = {}
 
         def row(tiles, u, j):
             return tiles[u // HALVES][:, (u % HALVES) * ROWS + j, :]
@@ -179,7 +184,7 @@ def tile_aattn_pb_kernel(tc, content, mean, std, out_w, out_b, out):
             nc.vector.reciprocal(out=inv_deviation[u][:], in_=deviation[u][:])
 
         def centre_times_std(u):
-            centred[u] = work.tile([P, ROWS, PIXELS], F32, name="centred", bufs=2)
+            centred[u] = work.tile([P, ROWS, PIXELS], F32, name="centred", bufs=4)
             for j in range(ROWS):
                 if u in VECTOR_STATS:
                     nc.vector.scalar_tensor_tensor(
@@ -198,6 +203,35 @@ def tile_aattn_pb_kernel(tc, content, mean, std, out_w, out_b, out):
                 nc.vector.scalar_tensor_tensor(
                     out=modulated[u][:, j, :], in0=centred[u][:, j, :], scalar=inv_deviation[u][:, j : j + 1],
                     in1=row(mean_sb, u, j), op0=ALU.mult, op1=ALU.add,
+                )
+
+        def tensor_scale_plus_mean(u):
+            diagonal = work.tile([P, ROWS, P], F32, name="diagonal", bufs=2)
+            for j in range(ROWS):
+                nc.scalar.activation(
+                    out=diagonal[:, j, :], in_=identity[:], func=ACT.Copy, scale=inv_deviation[u][:, j : j + 1]
+                )
+            summed[u] = []
+            first = (u % HALVES) * ROWS
+            for h in range(2):
+                bank = psum_o.tile([P, 2, PIXELS], F32, name="summed")
+                summed[u].append(bank)
+                nc.tensor.matmul(
+                    out=bank[:], lhsT=identity_bf[:],
+                    rhs=mean_sb[u // HALVES][:, first + 2 * h : first + 2 * h + 2, :],
+                    start=True, stop=False,
+                )
+                for e in range(2):
+                    nc.tensor.matmul(
+                        out=bank[:, e, :], lhsT=diagonal[:, 2 * h + e, :], rhs=centred[u][:, 2 * h + e, :],
+                        start=False, stop=(e == 1),
+                    )
+
+        def collect(u):
+            grouped[u] = work.tile([P, PIXELS, ROWS], BF16, name="grouped", align_bytes=64)
+            for h in range(2):
+                nc.scalar.copy(
+                    out=grouped[u][:, :, 2 * h : 2 * h + 2], in_=summed[u][h][:].rearrange("p e n -> p n e")
                 )
 
         def regroup(u):
@@ -269,7 +303,7 @@ def tile_aattn_pb_kernel(tc, content, mean, std, out_w, out_b, out):
                 quantise(i - 2)
             if on_vector(i + 2):
                 vector_partial_stats(i + 2)
-            if is_unit(i):
+            if is_unit(i) and i not in TENSOR_UNITS:
                 scale_plus_mean(i)
             if i in W_QUANTISE_STEPS:
                 w_quantise(W_QUANTISE_STEPS.index(i))
@@ -279,7 +313,12 @@ def tile_aattn_pb_kernel(tc, content, mean, std, out_w, out_b, out):
                 project(i - FINISH_LAG)
                 finish(i - FINISH_LAG)
             if is_unit(i - 1):
-                regroup(i - 1)
+                if i - 1 in TENSOR_UNITS:
+                    collect(i - 1)
+                else:
+                    regroup(i - 1)
+            if i in TENSOR_UNITS:
+                tensor_scale_plus_mean(i)
             if is_unit(i + 1):
                 scalar_deviation(i + 1)
             if on_scalar(i + 2):

@@ -26,7 +26,7 @@ EPS = 1e-5
 FLOPS = 2 * CHANNELS * CHANNELS * IMAGES * PIXELS
 
 VECTOR_STATS = (0, 2, 4, 6)
-W_QUANTISE_STEPS = (2, 4)
+W_QUANTISE_STEPS = (3, 5)
 FINISH_LAG = 4
 TENSOR_UNITS = (2, 4, 6)
 
@@ -56,10 +56,13 @@ def tile_aattn_pb_kernel(tc, content, mean, std, out_w, out_b, out):
 
         def load_content(b):
             for g in range(HALVES):
-                nc.sync.dma_start(
-                    out=x_sb[b][:, g * ROWS : (g + 1) * ROWS, :].rearrange("p j n -> p (j n)"),
-                    in_=x_dram[b][:, g, :],
-                )
+                pieces = 2 if (b, g) == (0, 0) else 1
+                rows = ROWS // pieces
+                for k in range(pieces):
+                    nc.sync.dma_start(
+                        out=x_sb[b][:, g * ROWS + k * rows : g * ROWS + (k + 1) * rows, :].rearrange("p j n -> p (j n)"),
+                        in_=x_dram[b][:, g, k * rows * PIXELS : (k + 1) * rows * PIXELS],
+                    )
 
         def load_image(tiles, dram, b):
             nc.sync.dma_start(out=tiles[b][:].rearrange("p (g j) n -> p g (j n)", g=HALVES), in_=dram[b])
@@ -272,6 +275,7 @@ def tile_aattn_pb_kernel(tc, content, mean, std, out_w, out_b, out):
         def finish(u):
             result = work.tile([P, ROWS, PIXELS], F32, name="result")
             for pair in range(ROWS // 2):
+                last = u == UNITS - 1 and pair == ROWS // 2 - 1
                 for side in range(2):
                     j = 2 * pair + side
                     nc.vector.scalar_tensor_tensor(
@@ -279,10 +283,15 @@ def tile_aattn_pb_kernel(tc, content, mean, std, out_w, out_b, out):
                         scalar=bias[:, (u % HALVES) * ROWS + j : (u % HALVES) * ROWS + j + 1],
                         in1=row(x_sb, u, j), op0=ALU.add, op1=ALU.add,
                     )
-                nc.sync.dma_start(
-                    out=out_dram[u // HALVES][:, u % HALVES, 2 * pair * PIXELS : 2 * (pair + 1) * PIXELS],
-                    in_=result[:, 2 * pair : 2 * (pair + 1), :].rearrange("p j n -> p (j n)"),
-                )
+                    if last:
+                        nc.sync.dma_start(
+                            out=out_dram[u // HALVES][:, u % HALVES, j * PIXELS : (j + 1) * PIXELS], in_=result[:, j, :]
+                        )
+                if not last:
+                    nc.sync.dma_start(
+                        out=out_dram[u // HALVES][:, u % HALVES, 2 * pair * PIXELS : 2 * (pair + 1) * PIXELS],
+                        in_=result[:, 2 * pair : 2 * (pair + 1), :].rearrange("p j n -> p (j n)"),
+                    )
 
         def is_unit(u):
             return 0 <= u < UNITS
@@ -325,8 +334,8 @@ def tile_aattn_pb_kernel(tc, content, mean, std, out_w, out_b, out):
                 scalar_minus_mu(i + 2)
             if on_scalar(i + 3):
                 scalar_total(i + 3)
-            if 0 <= 2 * i < TILES:
-                w_transpose(2 * i)
-                w_transpose(2 * i + 1)
+            if 0 <= 2 * (i - 1) < TILES:
+                w_transpose(2 * (i - 1))
+                w_transpose(2 * (i - 1) + 1)
             if on_scalar(i + 2):
                 scalar_squares(i + 2)

@@ -107,7 +107,6 @@ def tile_aattn_pb_kernel(tc, content, mean, std, out_w, out_b, out):
         partial = {u: keep.tile([P, ROWS, 6], F32, name="partial%d" % u) for u in VECTOR_STATS}
         mean_var = {u: keep.tile([P, ROWS, 2], F32, name="mean_var%d" % u) for u in VECTOR_STATS}
         scalar_units = [u for u in range(UNITS) if u not in VECTOR_STATS]
-        total = {u: keep.tile([P, ROWS], F32, name="total%d" % u) for u in scalar_units}
         minus_mu = {u: keep.tile([P, ROWS], F32, name="minus_mu%d" % u) for u in scalar_units}
         squares = {u: keep.tile([P, ROWS], F32, name="squares%d" % u) for u in scalar_units}
         deviation = [keep.tile([P, ROWS], F32, name="deviation%d" % u) for u in range(UNITS)]
@@ -157,12 +156,9 @@ def tile_aattn_pb_kernel(tc, content, mean, std, out_w, out_b, out):
         def scalar_total(u):
             for j in range(ROWS):
                 nc.scalar.activation(
-                    out=unread[:, j, :], in_=row(x_sb, u, j), func=ACT.Identity,
-                    accum_out=total[u][:, j : j + 1],
+                    out=unread[:, j, :], in_=row(x_sb, u, j), func=ACT.Identity, scale=-1.0 / PIXELS,
+                    accum_out=minus_mu[u][:, j : j + 1],
                 )
-
-        def scalar_minus_mu(u):
-            nc.scalar.mul(out=minus_mu[u][:], in_=total[u][:], mul=-1.0 / PIXELS)
 
         def scalar_squares(u):
             for j in range(ROWS):
@@ -330,8 +326,6 @@ def tile_aattn_pb_kernel(tc, content, mean, std, out_w, out_b, out):
                 tensor_scale_plus_mean(i)
             if is_unit(i + 1):
                 scalar_deviation(i + 1)
-            if on_scalar(i + 2):
-                scalar_minus_mu(i + 2)
             if on_scalar(i + 3):
                 scalar_total(i + 3)
             if 0 <= 2 * (i - 1) < TILES:

@@ -213,38 +213,42 @@ def tile_aattn_pb_kernel(tc, content, mean, std, out_w, out_b, out):
             summed[u] = []
             first = (u % HALVES) * ROWS
             for h in range(2):
-                bank = psum_o.tile([P, 2, PIXELS], F32, name="summed")
+                bank = psum_o.tile([P, ROWS, P], F32, name="summed")
                 summed[u].append(bank)
                 nc.tensor.matmul(
                     out=bank[:], lhsT=identity_bf[:],
-                    rhs=mean_sb[u // HALVES][:, first + 2 * h : first + 2 * h + 2, :],
+                    rhs=mean_sb[u // HALVES][:, first : first + ROWS, P * h : P * (h + 1)],
                     start=True, stop=False,
                 )
-                for e in range(2):
+            for j in range(ROWS):
+                for h in range(2):
                     nc.tensor.matmul(
-                        out=bank[:, e, :], lhsT=diagonal[:, 2 * h + e, :], rhs=centred[u][:, 2 * h + e, :],
-                        start=False, stop=(e == 1),
+                        out=summed[u][h][:, j, :], lhsT=diagonal[:, j, :], rhs=centred[u][:, j, P * h : P * (h + 1)],
+                        start=False, stop=(j == ROWS - 1),
                     )
 
+        def grouped_half(u):
+            if u // HALVES not in grouped:
+                grouped[u // HALVES] = work.tile([P, HALVES, PIXELS, ROWS], BF16, name="grouped", align_bytes=64)
+            return grouped[u // HALVES][:, u % HALVES, :, :]
+
         def collect(u):
-            grouped[u] = work.tile([P, PIXELS, ROWS], BF16, name="grouped", align_bytes=64)
             for h in range(2):
                 nc.scalar.copy(
-                    out=grouped[u][:, :, 2 * h : 2 * h + 2], in_=summed[u][h][:].rearrange("p e n -> p n e")
+                    out=grouped_half(u)[:, P * h : P * (h + 1), :], in_=summed[u][h][:].rearrange("p j n -> p n j")
                 )
 
         def regroup(u):
-            grouped[u] = work.tile([P, PIXELS, ROWS], BF16, name="grouped", align_bytes=64)
             nc.scalar.copy(
-                out=grouped[u][:].rearrange("p (c i) j -> p c j i", i=RUN),
+                out=grouped_half(u).rearrange("p (c i) j -> p c j i", i=RUN),
                 in_=modulated[u][:].rearrange("p j (c i) -> p c j i", i=RUN),
             )
 
-        def quantise(u):
+        def quantise(b):
             nc.vector.quantize_mx(
-                out=o_words[u // HALVES][:, u % HALVES, :].bitcast(FP8X4),
-                scales=o_scales[u // HALVES][:, u % HALVES, :],
-                in_=grouped[u][:].rearrange("p n j -> p (n j)"),
+                out=o_words[b][:].rearrange("p g n -> p (g n)").bitcast(FP8X4),
+                scales=o_scales[b][:].rearrange("p g n -> p (g n)"),
+                in_=grouped[b][:].rearrange("p g n j -> p (g n j)"),
             )
 
         def project(u):
@@ -304,8 +308,8 @@ def tile_aattn_pb_kernel(tc, content, mean, std, out_w, out_b, out):
                 vector_inverse(i)
             if on_vector(i + 1):
                 vector_mean_var(i + 1)
-            if is_unit(i - 2):
-                quantise(i - 2)
+            if is_unit(i - 2) and (i - 2) % HALVES == HALVES - 1:
+                quantise((i - 2) // HALVES)
             if on_vector(i + 2):
                 vector_partial_stats(i + 2)
             if is_unit(i) and i not in TENSOR_UNITS:

@@ -104,8 +104,7 @@ def tile_aattn_pb_kernel(tc, content, mean, std, out_w, out_b, out):
         o_words = [keep.tile([P, HALVES, PIXELS], U32, name="o_words%d" % b, align_bytes=64) for b in range(IMAGES)]
         o_scales = [keep.tile([P, HALVES, PIXELS], U8, name="o_scales%d" % b, align_bytes=64) for b in range(IMAGES)]
 
-        partial = {u: keep.tile([P, ROWS, 6], F32, name="partial%d" % u) for u in VECTOR_STATS}
-        mean_var = {u: keep.tile([P, ROWS, 2], F32, name="mean_var%d" % u) for u in VECTOR_STATS}
+        row_stats = {u: keep.tile([P, ROWS // 2, 6], F32, name="row_stats%d" % u) for u in VECTOR_STATS}
         scalar_units = [u for u in range(UNITS) if u not in VECTOR_STATS]
         minus_mu = {u: keep.tile([P, ROWS], F32, name="minus_mu%d" % u) for u in scalar_units}
         squares = {u: keep.tile([P, ROWS], F32, name="squares%d" % u) for u in scalar_units}
@@ -145,13 +144,13 @@ def tile_aattn_pb_kernel(tc, content, mean, std, out_w, out_b, out):
                     in_=w_grouped[:, g, ROWS * half : ROWS * (half + 1), :].rearrange("p t k -> p (t k)"),
                 )
 
-        def vector_partial_stats(u):
-            for j in range(ROWS):
-                nc.vector.bn_stats(out=partial[u][:, j, :], in_=row(x_sb, u, j))
-
-        def vector_mean_var(u):
-            for j in range(ROWS):
-                nc.vector.bn_aggr(out=mean_var[u][:, j, :], in_=partial[u][:, j, :])
+        def vector_stats(u):
+            first = (u % HALVES) * ROWS
+            for q in range(ROWS // 2):
+                nc.vector.bn_stats(
+                    out=row_stats[u][:, q, :],
+                    in_=x_sb[u // HALVES][:, first + 2 * q : first + 2 * q + 2, :].rearrange("p e n -> p n e"),
+                )
 
         def scalar_total(u):
             for j in range(ROWS):
@@ -170,8 +169,8 @@ def tile_aattn_pb_kernel(tc, content, mean, std, out_w, out_b, out):
         def scalar_deviation(u):
             if u in VECTOR_STATS:
                 nc.scalar.activation(
-                    out=deviation[u][:], in_=mean_var[u][:, :, 1], func=ACT.Sqrt,
-                    bias=eps[:], scale=float(PIXELS) / (PIXELS - 1),
+                    out=deviation[u][:].rearrange("p (q e) -> p q e", e=2), in_=row_stats[u][:, :, 2::3], func=ACT.Sqrt,
+                    bias=eps[:], scale=1.0 / (PIXELS - 1),
                 )
             else:
                 nc.scalar.activation(
@@ -187,7 +186,8 @@ def tile_aattn_pb_kernel(tc, content, mean, std, out_w, out_b, out):
             for j in range(ROWS):
                 if u in VECTOR_STATS:
                     nc.vector.scalar_tensor_tensor(
-                        out=centred[u][:, j, :], in0=row(x_sb, u, j), scalar=mean_var[u][:, j, 0:1],
+                        out=centred[u][:, j, :], in0=row(x_sb, u, j),
+                        scalar=row_stats[u][:, j // 2, 3 * (j % 2) + 1 : 3 * (j % 2) + 2],
                         in1=row(std_sb, u, j), op0=ALU.subtract, op1=ALU.mult,
                     )
                 else:
@@ -306,12 +306,10 @@ def tile_aattn_pb_kernel(tc, content, mean, std, out_w, out_b, out):
             if is_unit(i):
                 centre_times_std(i)
                 vector_inverse(i)
-            if on_vector(i + 1):
-                vector_mean_var(i + 1)
             if is_unit(i - 2) and (i - 2) % HALVES == HALVES - 1:
                 quantise((i - 2) // HALVES)
             if on_vector(i + 2):
-                vector_partial_stats(i + 2)
+                vector_stats(i + 2)
             if is_unit(i) and i not in TENSOR_UNITS:
                 scale_plus_mean(i)
             if i in W_QUANTISE_STEPS:

@@ -26,8 +26,6 @@ EPS = 1e-5
 FLOPS = 2 * CHANNELS * CHANNELS * IMAGES * PIXELS
 
 VECTOR_STATS = (0, 2, 4, 6)
-W_QUANTISE_STEPS = (3, 5)
-FINISH_LAG = 4
 TENSOR_UNITS = (2, 4, 6)
 
 
@@ -48,6 +46,8 @@ def tile_aattn_pb_kernel(tc, content, mean, std, out_w, out_b, out):
         psum_y = ctx.enter_context(tc.psum_pool(name="psum_y", bufs=4))
         psum_o = ctx.enter_context(tc.psum_pool(name="psum_o", bufs=2))
 
+        ctx.enter_context(tc.manual_schedule())
+
         x_sb = [keep.tile([P, TILES, PIXELS], BF16, name="x%d" % b) for b in range(IMAGES)]
         std_sb = [keep.tile([P, TILES, PIXELS], BF16, name="std%d" % b) for b in range(IMAGES)]
         mean_sb = [keep.tile([P, TILES, PIXELS], BF16, name="mean%d" % b) for b in range(IMAGES)]
@@ -67,20 +67,26 @@ def tile_aattn_pb_kernel(tc, content, mean, std, out_w, out_b, out):
         def load_image(tiles, dram, b):
             nc.sync.dma_start(out=tiles[b][:].rearrange("p (g j) n -> p g (j n)", g=HALVES), in_=dram[b])
 
+        def load_half(tiles, dram, b, g):
+            nc.sync.dma_start(
+                out=tiles[b][:, g * ROWS : (g + 1) * ROWS, :].rearrange("p j n -> p (j n)"), in_=dram[b][:, g, :]
+            )
+
         def load_w(q):
             nc.sync.dma_start(out=w_sb[q][:], in_=w_dram[q // 2, q % 2])
 
         load_content(0)
-        load_image(std_sb, std_dram, 0)
+        for g in range(HALVES):
+            load_half(std_sb, std_dram, 0, g)
         load_content(1)
         load_image(mean_sb, mean_dram, 0)
         load_w(0)
         load_image(std_sb, std_dram, 1)
         load_w(1)
-        load_image(mean_sb, mean_dram, 1)
         load_content(2)
-        load_w(2)
+        load_image(mean_sb, mean_dram, 1)
         load_image(std_sb, std_dram, 2)
+        load_w(2)
         load_w(3)
         nc.sync.dma_start(out=bias_bf[:], in_=bias_dram)
         load_image(mean_sb, mean_dram, 2)
@@ -117,6 +123,8 @@ def tile_aattn_pb_kernel(tc, content, mean, std, out_w, out_b, out):
         grouped = {}
         projected = {}
         summed = {}
+        transposed = {}
+        diagonal = {}
 
         def row(tiles, u, j):
             return tiles[u // HALVES][:, (u % HALVES) * ROWS + j, :]
@@ -131,10 +139,19 @@ def tile_aattn_pb_kernel(tc, content, mean, std, out_w, out_b, out):
                         in_=words[:, tile_index % 2, PASS_WORDS * g + e : PASS_WORDS * (g + 1) : 2],
                         identity=identity[:],
                     )
+            transposed[tile_index] = planes
+
+        def w_copy(tile_index):
             nc.scalar.copy(
                 out=w_grouped[:].bitcast(F32)[:, :, tile_index, :].rearrange("p g (m e) -> p g m e", e=2),
-                in_=planes[:].rearrange("p g e m -> p g m e"),
+                in_=transposed[tile_index][:].rearrange("p g e m -> p g m e"),
             )
+
+        def w_quarter(q):
+            for k in range(2):
+                w_transpose(2 * q + k)
+            for k in range(2):
+                w_copy(2 * q + k)
 
         def w_quantise(half):
             for g in range(HALVES):
@@ -204,26 +221,31 @@ def tile_aattn_pb_kernel(tc, content, mean, std, out_w, out_b, out):
                     in1=row(mean_sb, u, j), op0=ALU.mult, op1=ALU.add,
                 )
 
-        def tensor_scale_plus_mean(u):
-            diagonal = work.tile([P, ROWS, P], F32, name="diagonal", bufs=2)
+        def diagonals(u):
+            diagonal[u] = work.tile([P, ROWS, P], F32, name="diagonal", bufs=2)
             for j in range(ROWS):
                 nc.scalar.activation(
-                    out=diagonal[:, j, :], in_=identity[:], func=ACT.Copy, scale=inv_deviation[u][:, j : j + 1]
+                    out=diagonal[u][:, j, :], in_=identity[:], func=ACT.Copy, scale=inv_deviation[u][:, j : j + 1]
                 )
+
+        def tensor_scale_plus_mean(u):
             summed[u] = []
             first = (u % HALVES) * ROWS
             for h in range(2):
-                bank = psum_o.tile([P, ROWS, P], F32, name="summed")
+                if u == TENSOR_UNITS[-1]:
+                    bank = psum_w.tile([P, ROWS, P], F32, name="summed", tag="planes")
+                else:
+                    bank = psum_o.tile([P, ROWS, P], F32, name="summed")
                 summed[u].append(bank)
                 nc.tensor.matmul(
                     out=bank[:], lhsT=identity_bf[:],
                     rhs=mean_sb[u // HALVES][:, first : first + ROWS, P * h : P * (h + 1)],
                     start=True, stop=False,
                 )
-            for j in range(ROWS):
-                for h in range(2):
+            for h in range(2):
+                for j in range(ROWS):
                     nc.tensor.matmul(
-                        out=summed[u][h][:, j, :], lhsT=diagonal[:, j, :], rhs=centred[u][:, j, P * h : P * (h + 1)],
+                        out=summed[u][h][:, j, :], lhsT=diagonal[u][:, j, :], rhs=centred[u][:, j, P * h : P * (h + 1)],
                         start=False, stop=(j == ROWS - 1),
                     )
 
@@ -293,45 +315,66 @@ def tile_aattn_pb_kernel(tc, content, mean, std, out_w, out_b, out):
                         in_=result[:, 2 * pair : 2 * (pair + 1), :].rearrange("p j n -> p (j n)"),
                     )
 
-        def is_unit(u):
-            return 0 <= u < UNITS
+        def scalar_stats(u):
+            scalar_total(u)
+            scalar_deviation(u - 1)
+            scalar_squares(u)
+            scalar_deviation(u)
 
-        def on_vector(u):
-            return is_unit(u) and u in VECTOR_STATS
-
-        def on_scalar(u):
-            return is_unit(u) and u not in VECTOR_STATS
-
-        for i in range(-3, UNITS + FINISH_LAG):
-            if is_unit(i):
-                centre_times_std(i)
-                vector_inverse(i)
-            if is_unit(i - 2) and (i - 2) % HALVES == HALVES - 1:
-                quantise((i - 2) // HALVES)
-            if on_vector(i + 2):
-                vector_stats(i + 2)
-            if is_unit(i) and i not in TENSOR_UNITS:
-                scale_plus_mean(i)
-            if i in W_QUANTISE_STEPS:
-                w_quantise(W_QUANTISE_STEPS.index(i))
-            if i == FINISH_LAG:
+        vector_stats(0)
+        scalar_stats(1)
+        for b in range(IMAGES):
+            even, odd = HALVES * b, HALVES * b + 1
+            centre_times_std(even)
+            vector_inverse(even)
+            if b == 3:
+                w_quantise(1)
+            centre_times_std(odd)
+            if b < IMAGES - 1:
+                vector_stats(even + HALVES)
+            vector_inverse(odd)
+            if even in TENSOR_UNITS:
+                diagonals(even)
+            if b == 1:
+                w_quarter(1)
+            if b == 2:
+                project(0)
+                w_quarter(3)
+            if b == 3:
+                project(2)
+                project(1)
+            if even in TENSOR_UNITS:
+                tensor_scale_plus_mean(even)
+            if b == 3:
+                collect(4)
+            if b == 2:
                 nc.vector.tensor_copy(out=bias[:], in_=bias_bf[:].rearrange("p g j -> p (g j)"))
-            if is_unit(i - FINISH_LAG):
-                project(i - FINISH_LAG)
-                finish(i - FINISH_LAG)
-            if is_unit(i - 1):
-                if i - 1 in TENSOR_UNITS:
-                    collect(i - 1)
-                else:
-                    regroup(i - 1)
-            if i in TENSOR_UNITS:
-                tensor_scale_plus_mean(i)
-            if is_unit(i + 1):
-                scalar_deviation(i + 1)
-            if on_scalar(i + 3):
-                scalar_total(i + 3)
-            if 0 <= 2 * (i - 1) < TILES:
-                w_transpose(2 * (i - 1))
-                w_transpose(2 * (i - 1) + 1)
-            if on_scalar(i + 2):
-                scalar_squares(i + 2)
+                finish(0)
+            if b == 3:
+                finish(2)
+                finish(1)
+            if b > 0:
+                quantise(b - 1)
+            if even not in TENSOR_UNITS:
+                scale_plus_mean(even)
+            scale_plus_mean(odd)
+            if b == 1:
+                w_quantise(0)
+            if b < IMAGES - 1:
+                scalar_stats(odd + HALVES)
+            if b == 3:
+                collect(6)
+            if even not in TENSOR_UNITS:
+                regroup(even)
+            regroup(odd)
+            if b < 2:
+                w_quarter(2 * b)
+            if b == 1:
+                collect(2)
+        for u in (3, 4):
+            project(u)
+            finish(u)
+        quantise(3)
+        for u in (5, 6, 7):
+            project(u)
+            finish(u)

@@ -42,8 +42,7 @@ def tile_aattn_pb_kernel(tc, content, mean, std, out_w, out_b, out):
     with ExitStack() as ctx:
         keep = ctx.enter_context(tc.tile_pool(name="keep", bufs=1))
         work = ctx.enter_context(tc.tile_pool(name="work", bufs=3))
-        psum_w = ctx.enter_context(tc.psum_pool(name="psum_w", bufs=2))
-        psum_y = ctx.enter_context(tc.psum_pool(name="psum_y", bufs=4))
+        psum_y = ctx.enter_context(tc.psum_pool(name="psum_y", bufs=6))
         psum_o = ctx.enter_context(tc.psum_pool(name="psum_o", bufs=2))
 
         ctx.enter_context(tc.manual_schedule())
@@ -131,7 +130,7 @@ def tile_aattn_pb_kernel(tc, content, mean, std, out_w, out_b, out):
 
         def w_transpose(tile_index):
             words = w_sb[tile_index // 2][:].bitcast(F32)
-            planes = psum_w.tile([P, HALVES, 2, P], F32, name="planes")
+            planes = psum_y.tile([P, HALVES, 2, P], F32, name="planes", tag="bank")
             for g in range(HALVES):
                 for e in range(2):
                     nc.tensor.transpose(
@@ -232,10 +231,7 @@ def tile_aattn_pb_kernel(tc, content, mean, std, out_w, out_b, out):
             summed[u] = []
             first = (u % HALVES) * ROWS
             for h in range(2):
-                if u == TENSOR_UNITS[-1]:
-                    bank = psum_w.tile([P, ROWS, P], F32, name="summed", tag="planes")
-                else:
-                    bank = psum_o.tile([P, ROWS, P], F32, name="summed")
+                bank = psum_o.tile([P, ROWS, P], F32, name="summed")
                 summed[u].append(bank)
                 nc.tensor.matmul(
                     out=bank[:], lhsT=identity_bf[:],
@@ -343,12 +339,11 @@ def tile_aattn_pb_kernel(tc, content, mean, std, out_w, out_b, out):
             if b == 3:
                 project(2)
                 project(1)
+                project(3)
+                collect(4)
             if even in TENSOR_UNITS:
                 tensor_scale_plus_mean(even)
-            if b == 3:
-                collect(4)
             if b == 2:
-                nc.vector.tensor_copy(out=bias[:], in_=bias_bf[:].rearrange("p g j -> p (g j)"))
                 finish(0)
             if b == 3:
                 finish(2)
@@ -360,6 +355,7 @@ def tile_aattn_pb_kernel(tc, content, mean, std, out_w, out_b, out):
             scale_plus_mean(odd)
             if b == 1:
                 w_quantise(0)
+                nc.vector.tensor_copy(out=bias[:], in_=bias_bf[:].rearrange("p g j -> p (g j)"))
             if b < IMAGES - 1:
                 scalar_stats(odd + HALVES)
             if b == 3:
@@ -371,9 +367,9 @@ def tile_aattn_pb_kernel(tc, content, mean, std, out_w, out_b, out):
                 w_quarter(2 * b)
             if b == 1:
                 collect(2)
-        for u in (3, 4):
-            project(u)
-            finish(u)
+        finish(3)
+        project(4)
+        finish(4)
         quantise(3)
         for u in (5, 6, 7):
             project(u)

@@ -25,7 +25,7 @@ TILES = HALVES * ROWS
 EPS = 1e-5
 FLOPS = 2 * CHANNELS * CHANNELS * IMAGES * PIXELS
 
-VECTOR_STATS = (0, 2, 4, 6)
+VECTOR_PAIRS = ((0, 0), (0, 1), (2, 0), (2, 1), (4, 0), (4, 1), (6, 0))
 TENSOR_UNITS = (2, 4, 6)
 
 
@@ -103,18 +103,19 @@ def tile_aattn_pb_kernel(tc, content, mean, std, out_w, out_b, out):
         nc.scalar.activation(out=first_sqrt[:], in_=eps[:], func=ACT.Sqrt)
         bias = keep.tile([P, TILES], F32, name="bias")
 
-        w_grouped = keep.tile([P, HALVES, TILES, ROWS * P], BF16, name="w_grouped", align_bytes=64)
-        w_words = keep.tile([P, HALVES, CHANNELS], U32, name="w_words", align_bytes=64)
-        w_scales = keep.tile([P, HALVES, CHANNELS], U8, name="w_scales", align_bytes=64)
+        w_grouped = keep.tile([P, 2, HALVES, ROWS, ROWS * P], BF16, name="w_grouped", align_bytes=64)
+        w_words = keep.tile([P, 2, HALVES, HALF], U32, name="w_words", align_bytes=64)
+        w_scales = keep.tile([P, 2, HALVES, HALF], U8, name="w_scales", align_bytes=64)
         o_words = [keep.tile([P, HALVES, PIXELS], U32, name="o_words%d" % b, align_bytes=64) for b in range(IMAGES)]
         o_scales = [keep.tile([P, HALVES, PIXELS], U8, name="o_scales%d" % b, align_bytes=64) for b in range(IMAGES)]
 
-        row_stats = {u: keep.tile([P, ROWS // 2, 6], F32, name="row_stats%d" % u) for u in VECTOR_STATS}
-        scalar_units = [u for u in range(UNITS) if u not in VECTOR_STATS]
-        minus_mu = {u: keep.tile([P, ROWS], F32, name="minus_mu%d" % u) for u in scalar_units}
-        squares = {u: keep.tile([P, ROWS], F32, name="squares%d" % u) for u in scalar_units}
-        deviation = [keep.tile([P, ROWS], F32, name="deviation%d" % u) for u in range(UNITS)]
-        inv_deviation = [keep.tile([P, ROWS], F32, name="inv_deviation%d" % u) for u in range(UNITS)]
+        row_stats = [keep.tile([P, ROWS // 2, 6], F32, name="row_stats%d" % u) for u in range(UNITS)]
+        minus_mu = [keep.tile([P, ROWS], F32, name="minus_mu%d" % u) for u in range(UNITS)]
+        squares = [keep.tile([P, ROWS], F32, name="squares%d" % u) for u in range(UNITS)]
+        deviations = [keep.tile([P, HALVES * ROWS], F32, name="deviations%d" % b) for b in range(IMAGES)]
+        inverses = [keep.tile([P, HALVES * ROWS], F32, name="inverses%d" % b) for b in range(IMAGES)]
+        deviation = [deviations[u // HALVES][:, (u % HALVES) * ROWS : (u % HALVES + 1) * ROWS] for u in range(UNITS)]
+        inv_deviation = [inverses[u // HALVES][:, (u % HALVES) * ROWS : (u % HALVES + 1) * ROWS] for u in range(UNITS)]
         unread = keep.tile([P, 2 * ROWS, PIXELS], BF16, name="unread")
 
         centred = {}
@@ -124,6 +125,12 @@ def tile_aattn_pb_kernel(tc, content, mean, std, out_w, out_b, out):
         summed = {}
         transposed = {}
         diagonal = {}
+
+        def vector_pairs(u):
+            return [q for q in range(ROWS // 2) if (u, q) in VECTOR_PAIRS]
+
+        def scalar_rows(u):
+            return [j for j in range(ROWS) if (u, j // 2) not in VECTOR_PAIRS]
 
         def row(tiles, u, j):
             return tiles[u // HALVES][:, (u % HALVES) * ROWS + j, :]
@@ -142,7 +149,9 @@ def tile_aattn_pb_kernel(tc, content, mean, std, out_w, out_b, out):
 
         def w_copy(tile_index):
             nc.scalar.copy(
-                out=w_grouped[:].bitcast(F32)[:, :, tile_index, :].rearrange("p g (m e) -> p g m e", e=2),
+                out=w_grouped[:].bitcast(F32)[:, tile_index // ROWS, :, tile_index % ROWS, :].rearrange(
+                    "p g (m e) -> p g m e", e=2
+                ),
                 in_=transposed[tile_index][:].rearrange("p g e m -> p g m e"),
             )
 
@@ -153,54 +162,58 @@ def tile_aattn_pb_kernel(tc, content, mean, std, out_w, out_b, out):
                 w_copy(2 * q + k)
 
         def w_quantise(half):
-            for g in range(HALVES):
-                nc.vector.quantize_mx(
-                    out=w_words[:, g, HALF * half : HALF * (half + 1)].bitcast(FP8X4),
-                    scales=w_scales[:, g, HALF * half : HALF * (half + 1)],
-                    in_=w_grouped[:, g, ROWS * half : ROWS * (half + 1), :].rearrange("p t k -> p (t k)"),
-                )
+            nc.vector.quantize_mx(
+                out=w_words[:, half].rearrange("p g m -> p (g m)").bitcast(FP8X4),
+                scales=w_scales[:, half].rearrange("p g m -> p (g m)"),
+                in_=w_grouped[:, half].rearrange("p g t k -> p (g t k)"),
+            )
 
         def vector_stats(u):
             first = (u % HALVES) * ROWS
-            for q in range(ROWS // 2):
+            for q in vector_pairs(u):
                 nc.vector.bn_stats(
                     out=row_stats[u][:, q, :],
                     in_=x_sb[u // HALVES][:, first + 2 * q : first + 2 * q + 2, :].rearrange("p e n -> p n e"),
                 )
 
         def scalar_total(u):
-            for j in range(ROWS):
+            for j in scalar_rows(u):
                 nc.scalar.activation(
                     out=unread[:, j, :], in_=row(x_sb, u, j), func=ACT.Identity, scale=-1.0 / PIXELS,
                     accum_out=minus_mu[u][:, j : j + 1],
                 )
 
         def scalar_squares(u):
-            for j in range(ROWS):
+            for j in scalar_rows(u):
                 nc.scalar.activation(
                     out=unread[:, ROWS + j, :], in_=row(x_sb, u, j), func=ACT.Square,
                     bias=minus_mu[u][:, j : j + 1], accum_out=squares[u][:, j : j + 1],
                 )
 
         def scalar_deviation(u):
-            if u in VECTOR_STATS:
+            pairs, rows = vector_pairs(u), scalar_rows(u)
+            if pairs:
                 nc.scalar.activation(
-                    out=deviation[u][:].rearrange("p (q e) -> p q e", e=2), in_=row_stats[u][:, :, 2::3], func=ACT.Sqrt,
+                    out=deviation[u][:, 0 : 2 * len(pairs)].rearrange("p (q e) -> p q e", e=2),
+                    in_=row_stats[u][:, 0 : len(pairs), 2::3], func=ACT.Sqrt,
                     bias=eps[:], scale=1.0 / (PIXELS - 1),
                 )
-            else:
+            if rows:
                 nc.scalar.activation(
-                    out=deviation[u][:], in_=squares[u][:], func=ACT.Sqrt,
+                    out=deviation[u][:, rows[0] : ROWS], in_=squares[u][:, rows[0] : ROWS], func=ACT.Sqrt,
                     bias=eps[:], scale=1.0 / (PIXELS - 1),
                 )
 
         def vector_inverse(u):
-            nc.vector.reciprocal(out=inv_deviation[u][:], in_=deviation[u][:])
+            nc.vector.reciprocal(out=inv_deviation[u], in_=deviation[u])
+
+        def vector_inverses(b):
+            nc.vector.reciprocal(out=inverses[b][:], in_=deviations[b][:])
 
         def centre_times_std(u):
             centred[u] = work.tile([P, ROWS, PIXELS], F32, name="centred", bufs=4)
             for j in range(ROWS):
-                if u in VECTOR_STATS:
+                if (u, j // 2) in VECTOR_PAIRS:
                     nc.vector.scalar_tensor_tensor(
                         out=centred[u][:, j, :], in0=row(x_sb, u, j),
                         scalar=row_stats[u][:, j // 2, 3 * (j % 2) + 1 : 3 * (j % 2) + 2],
@@ -276,14 +289,12 @@ def tile_aattn_pb_kernel(tc, content, mean, std, out_w, out_b, out):
                 bank = psum_y.tile([P, 2, PIXELS], F32, name="bank")
                 projected[u].append(bank)
                 for side in range(2):
-                    columns = slice(
-                        P * ((u % HALVES) * ROWS + 2 * pair + side), P * ((u % HALVES) * ROWS + 2 * pair + side + 1)
-                    )
+                    columns = slice(P * (2 * pair + side), P * (2 * pair + side + 1))
                     for g in range(HALVES):
                         nc.tensor.matmul_mx(
                             out=bank[:, side, :],
-                            lhsT=w_words[:, g, columns].bitcast(FP8X4),
-                            lhsT_scale=w_scales[:, g, columns],
+                            lhsT=w_words[:, u % HALVES, g, columns].bitcast(FP8X4),
+                            lhsT_scale=w_scales[:, u % HALVES, g, columns],
                             rhs=o_words[b][:, g, :].bitcast(FP8X4),
                             rhs_scale=o_scales[b][:, g, :],
                             start=(g == 0),
@@ -312,23 +323,32 @@ def tile_aattn_pb_kernel(tc, content, mean, std, out_w, out_b, out):
                     )
 
         def scalar_stats(u):
-            scalar_total(u)
-            scalar_deviation(u - 1)
-            scalar_squares(u)
+            if scalar_rows(u):
+                scalar_total(u)
+                scalar_squares(u)
             scalar_deviation(u)
 
         vector_stats(0)
-        scalar_stats(1)
+        scalar_total(1)
+        scalar_deviation(0)
+        scalar_squares(1)
+        scalar_deviation(1)
         for b in range(IMAGES):
             even, odd = HALVES * b, HALVES * b + 1
             centre_times_std(even)
-            vector_inverse(even)
             if b == 3:
                 w_quantise(1)
             centre_times_std(odd)
-            if b < IMAGES - 1:
+            if b == 0:
+                vector_stats(2)
+            if b == 3:
+                vector_inverse(even)
+            if b < 3:
+                vector_inverses(b)
+            if b in (1, 2):
                 vector_stats(even + HALVES)
-            vector_inverse(odd)
+            if b == 3:
+                collect(4)
             if even in TENSOR_UNITS:
                 diagonals(even)
             if b == 1:
@@ -337,10 +357,10 @@ def tile_aattn_pb_kernel(tc, content, mean, std, out_w, out_b, out):
                 project(0)
                 w_quarter(3)
             if b == 3:
+                regroup(5)
                 project(2)
                 project(1)
                 project(3)
-                collect(4)
             if even in TENSOR_UNITS:
                 tensor_scale_plus_mean(even)
             if b == 2:
@@ -348,25 +368,35 @@ def tile_aattn_pb_kernel(tc, content, mean, std, out_w, out_b, out):
             if b == 3:
                 finish(2)
                 finish(1)
+                vector_inverse(odd)
+                scale_plus_mean(odd)
             if b > 0:
                 quantise(b - 1)
             if even not in TENSOR_UNITS:
                 scale_plus_mean(even)
-            scale_plus_mean(odd)
+            if b < 3:
+                scale_plus_mean(odd)
             if b == 1:
                 w_quantise(0)
                 nc.vector.tensor_copy(out=bias[:], in_=bias_bf[:].rearrange("p g j -> p (g j)"))
-            if b < IMAGES - 1:
-                scalar_stats(odd + HALVES)
-            if b == 3:
-                collect(6)
-            if even not in TENSOR_UNITS:
-                regroup(even)
-            regroup(odd)
             if b < 2:
-                w_quarter(2 * b)
+                scalar_total(odd + HALVES)
+                scalar_deviation(even + HALVES)
+                scalar_squares(odd + HALVES)
+                scalar_deviation(odd + HALVES)
+            if b == 2:
+                scalar_stats(6)
+                scalar_stats(7)
             if b == 1:
                 collect(2)
+            if even not in TENSOR_UNITS:
+                regroup(even)
+            if b != 2:
+                regroup(odd)
+            if b == 3:
+                collect(6)
+            if b < 2:
+                w_quarter(2 * b)
         finish(3)
         project(4)
         finish(4)

@@ -302,7 +302,7 @@ def tile_aattn_pb_kernel(tc, content, mean, std, out_w, out_b, out):
                         )
 
         def finish(u):
-            result = work.tile([P, ROWS, PIXELS], F32, name="result")
+            result = work.tile([P, ROWS, PIXELS], F32, name="result", bufs=UNITS)
             for pair in range(ROWS // 2):
                 last = u == UNITS - 1 and pair == ROWS // 2 - 1
                 for side in range(2):
@@ -339,13 +339,10 @@ def tile_aattn_pb_kernel(tc, content, mean, std, out_w, out_b, out):
             if b == 3:
                 w_quantise(1)
             centre_times_std(odd)
-            if b == 0:
-                vector_stats(2)
             if b == 3:
                 vector_inverse(even)
             if b < 3:
                 vector_inverses(b)
-            if b in (1, 2):
                 vector_stats(even + HALVES)
             if b == 3:
                 collect(4)
@@ -367,8 +364,8 @@ def tile_aattn_pb_kernel(tc, content, mean, std, out_w, out_b, out):
                 finish(0)
             if b == 3:
                 finish(2)
-                finish(1)
                 vector_inverse(odd)
+                finish(1)
                 scale_plus_mean(odd)
             if b > 0:
                 quantise(b - 1)

from contextlib import ExitStack

import concourse.mybir as mybir
from concourse.masks import make_identity

F32 = mybir.dt.float32
BF16 = mybir.dt.bfloat16
U32 = mybir.dt.uint32
U8 = mybir.dt.uint8
FP8X4 = mybir.dt.float8_e4m3fn_x4
ALU = mybir.AluOpType
ACT = mybir.ActivationFunctionType

IMAGES = 4
CHANNELS = 1024
PIXELS = 256
P = 128
HALVES = 2
ROWS = 4
HALF = ROWS * P
PASS_WORDS = HALF // 2
RUN = 4
UNITS = IMAGES * HALVES
TILES = HALVES * ROWS
EPS = 1e-5
FLOPS = 2 * CHANNELS * CHANNELS * IMAGES * PIXELS

VECTOR_PAIRS = ((0, 0), (0, 1), (2, 0), (2, 1), (4, 0), (4, 1), (6, 0))
TENSOR_UNITS = (2, 4, 6)


def tile_aattn_pb_kernel(tc, content, mean, std, out_w, out_b, out):
    nc = tc.nc
    by_partition = "b (g p j) h w -> b p g (j h w)"
    x_dram = content.rearrange(by_partition, g=HALVES, p=P, j=ROWS)
    mean_dram = mean.rearrange(by_partition, g=HALVES, p=P, j=ROWS)
    std_dram = std.rearrange(by_partition, g=HALVES, p=P, j=ROWS)
    out_dram = out.rearrange(by_partition, g=HALVES, p=P, j=ROWS)
    w_dram = out_w.rearrange("(g p h j) k -> g h p j k", g=HALVES, p=P, h=2, j=2)
    bias_dram = out_b.rearrange("(g p j) -> p g j", g=HALVES, p=P, j=ROWS)

    with ExitStack() as ctx:
        keep = ctx.enter_context(tc.tile_pool(name="keep", bufs=1))
        work = ctx.enter_context(tc.tile_pool(name="work", bufs=3))
        psum_y = ctx.enter_context(tc.psum_pool(name="psum_y", bufs=6))
        psum_o = ctx.enter_context(tc.psum_pool(name="psum_o", bufs=2))

        ctx.enter_context(tc.manual_schedule())

        x_sb = [keep.tile([P, TILES, PIXELS], BF16, name="x%d" % b) for b in range(IMAGES)]
        std_sb = [keep.tile([P, TILES, PIXELS], BF16, name="std%d" % b) for b in range(IMAGES)]
        mean_sb = [keep.tile([P, TILES, PIXELS], BF16, name="mean%d" % b) for b in range(IMAGES)]
        w_sb = [keep.tile([P, 2, CHANNELS], BF16, name="w%d" % q) for q in range(4)]
        bias_bf = keep.tile([P, HALVES, ROWS], BF16, name="bias_bf")

        def load_content(b):
            for g in range(HALVES):
                pieces = 2 if (b, g) == (0, 0) else 1
                rows = ROWS // pieces
                for k in range(pieces):
                    nc.sync.dma_start(
                        out=x_sb[b][:, g * ROWS + k * rows : g * ROWS + (k + 1) * rows, :].rearrange("p j n -> p (j n)"),
                        in_=x_dram[b][:, g, k * rows * PIXELS : (k + 1) * rows * PIXELS],
                    )

        def load_image(tiles, dram, b):
            nc.sync.dma_start(out=tiles[b][:].rearrange("p (g j) n -> p g (j n)", g=HALVES), in_=dram[b])

        def load_half(tiles, dram, b, g):
            nc.sync.dma_start(
                out=tiles[b][:, g * ROWS : (g + 1) * ROWS, :].rearrange("p j n -> p (j n)"), in_=dram[b][:, g, :]
            )

        def load_w(q):
            nc.sync.dma_start(out=w_sb[q][:], in_=w_dram[q // 2, q % 2])

        load_content(0)
        for g in range(HALVES):
            load_half(std_sb, std_dram, 0, g)
        load_content(1)
        load_image(mean_sb, mean_dram, 0)
        load_w(0)
        load_image(std_sb, std_dram, 1)
        load_w(1)
        load_content(2)
        load_image(mean_sb, mean_dram, 1)
        load_image(std_sb, std_dram, 2)
        load_w(2)
        load_w(3)
        nc.sync.dma_start(out=bias_bf[:], in_=bias_dram)
        load_image(mean_sb, mean_dram, 2)
        load_content(3)
        load_image(std_sb, std_dram, 3)
        load_image(mean_sb, mean_dram, 3)

        identity = keep.tile([P, P], F32, name="identity")
        make_identity(nc, identity[:])
        identity_bf = keep.tile([P, P], BF16, name="identity_bf")
        make_identity(nc, identity_bf[:])
        eps = keep.tile([P, 1], F32, name="eps")
        nc.vector.memset(eps[:], EPS)
        first_sqrt = keep.tile([P, 1], F32, name="first_sqrt")
        nc.scalar.activation(out=first_sqrt[:], in_=eps[:], func=ACT.Sqrt)
        bias = keep.tile([P, TILES], F32, name="bias")

        w_grouped = keep.tile([P, 2, HALVES, ROWS, ROWS * P], BF16, name="w_grouped", align_bytes=64)
        w_words = keep.tile([P, 2, HALVES, HALF], U32, name="w_words", align_bytes=64)
        w_scales = keep.tile([P, 2, HALVES, HALF], U8, name="w_scales", align_bytes=64)
        o_words = [keep.tile([P, HALVES, PIXELS], U32, name="o_words%d" % b, align_bytes=64) for b in range(IMAGES)]
        o_scales = [keep.tile([P, HALVES, PIXELS], U8, name="o_scales%d" % b, align_bytes=64) for b in range(IMAGES)]

        row_stats = [keep.tile([P, ROWS // 2, 6], F32, name="row_stats%d" % u) for u in range(UNITS)]
        minus_mu = [keep.tile([P, ROWS], F32, name="minus_mu%d" % u) for u in range(UNITS)]
        squares = [keep.tile([P, ROWS], F32, name="squares%d" % u) for u in range(UNITS)]
        deviations = [keep.tile([P, HALVES * ROWS], F32, name="deviations%d" % b) for b in range(IMAGES)]
        inverses = [keep.tile([P, HALVES * ROWS], F32, name="inverses%d" % b) for b in range(IMAGES)]
        deviation = [deviations[u // HALVES][:, (u % HALVES) * ROWS : (u % HALVES + 1) * ROWS] for u in range(UNITS)]
        inv_deviation = [inverses[u // HALVES][:, (u % HALVES) * ROWS : (u % HALVES + 1) * ROWS] for u in range(UNITS)]
        unread = keep.tile([P, 2 * ROWS, PIXELS], BF16, name="unread")

        centred = {}
        modulated = {}
        grouped = {}
        projected = {}
        summed = {}
        transposed = {}
        diagonal = {}

        def vector_pairs(u):
            return [q for q in range(ROWS // 2) if (u, q) in VECTOR_PAIRS]

        def scalar_rows(u):
            return [j for j in range(ROWS) if (u, j // 2) not in VECTOR_PAIRS]

        def row(tiles, u, j):
            return tiles[u // HALVES][:, (u % HALVES) * ROWS + j, :]

        def w_transpose(tile_index):
            words = w_sb[tile_index // 2][:].bitcast(F32)
            planes = psum_y.tile([P, HALVES, 2, P], F32, name="planes", tag="bank")
            for g in range(HALVES):
                for e in range(2):
                    nc.tensor.transpose(
                        out=planes[:, g, e, :],
                        in_=words[:, tile_index % 2, PASS_WORDS * g + e : PASS_WORDS * (g + 1) : 2],
                        identity=identity[:],
                    )
            transposed[tile_index] = planes

        def w_copy(tile_index):
            nc.scalar.copy(
                out=w_grouped[:].bitcast(F32)[:, tile_index // ROWS, :, tile_index % ROWS, :].rearrange(
                    "p g (m e) -> p g m e", e=2
                ),
                in_=transposed[tile_index][:].rearrange("p g e m -> p g m e"),
            )

        def w_quarter(q):
            for k in range(2):
                w_transpose(2 * q + k)
            for k in range(2):
                w_copy(2 * q + k)

        def w_quantise(half):
            nc.vector.quantize_mx(
                out=w_words[:, half].rearrange("p g m -> p (g m)").bitcast(FP8X4),
                scales=w_scales[:, half].rearrange("p g m -> p (g m)"),
                in_=w_grouped[:, half].rearrange("p g t k -> p (g t k)"),
            )

        def vector_stats(u):
            first = (u % HALVES) * ROWS
            for q in vector_pairs(u):
                nc.vector.bn_stats(
                    out=row_stats[u][:, q, :],
                    in_=x_sb[u // HALVES][:, first + 2 * q : first + 2 * q + 2, :].rearrange("p e n -> p n e"),
                )

        def scalar_total(u):
            for j in scalar_rows(u):
                nc.scalar.activation(
                    out=unread[:, j, :], in_=row(x_sb, u, j), func=ACT.Identity, scale=-1.0 / PIXELS,
                    accum_out=minus_mu[u][:, j : j + 1],
                )

        def scalar_squares(u):
            for j in scalar_rows(u):
                nc.scalar.activation(
                    out=unread[:, ROWS + j, :], in_=row(x_sb, u, j), func=ACT.Square,
                    bias=minus_mu[u][:, j : j + 1], accum_out=squares[u][:, j : j + 1],
                )

        def scalar_deviation(u):
            pairs, rows = vector_pairs(u), scalar_rows(u)
            if pairs:
                nc.scalar.activation(
                    out=deviation[u][:, 0 : 2 * len(pairs)].rearrange("p (q e) -> p q e", e=2),
                    in_=row_stats[u][:, 0 : len(pairs), 2::3], func=ACT.Sqrt,
                    bias=eps[:], scale=1.0 / (PIXELS - 1),
                )
            if rows:
                nc.scalar.activation(
                    out=deviation[u][:, rows[0] : ROWS], in_=squares[u][:, rows[0] : ROWS], func=ACT.Sqrt,
                    bias=eps[:], scale=1.0 / (PIXELS - 1),
                )

        def vector_inverse(u):
            nc.vector.reciprocal(out=inv_deviation[u], in_=deviation[u])

        def vector_inverses(b):
            nc.vector.reciprocal(out=inverses[b][:], in_=deviations[b][:])

        def centre_times_std(u):
            centred[u] = work.tile([P, ROWS, PIXELS], F32, name="centred", bufs=4)
            for j in range(ROWS):
                if (u, j // 2) in VECTOR_PAIRS:
                    nc.vector.scalar_tensor_tensor(
                        out=centred[u][:, j, :], in0=row(x_sb, u, j),
                        scalar=row_stats[u][:, j // 2, 3 * (j % 2) + 1 : 3 * (j % 2) + 2],
                        in1=row(std_sb, u, j), op0=ALU.subtract, op1=ALU.mult,
                    )
                else:
                    nc.vector.scalar_tensor_tensor(
                        out=centred[u][:, j, :], in0=row(x_sb, u, j), scalar=minus_mu[u][:, j : j + 1],
                        in1=row(std_sb, u, j), op0=ALU.add, op1=ALU.mult,
                    )

        def scale_plus_mean(u):
            modulated[u] = work.tile([P, ROWS, PIXELS], BF16, name="modulated")
            for j in range(ROWS):
                nc.vector.scalar_tensor_tensor(
                    out=modulated[u][:, j, :], in0=centred[u][:, j, :], scalar=inv_deviation[u][:, j : j + 1],
                    in1=row(mean_sb, u, j), op0=ALU.mult, op1=ALU.add,
                )

        def diagonals(u):
            diagonal[u] = work.tile([P, ROWS, P], F32, name="diagonal", bufs=2)
            for j in range(ROWS):
                nc.scalar.activation(
                    out=diagonal[u][:, j, :], in_=identity[:], func=ACT.Copy, scale=inv_deviation[u][:, j : j + 1]
                )

        def tensor_scale_plus_mean(u):
            summed[u] = []
            first = (u % HALVES) * ROWS
            for h in range(2):
                bank = psum_o.tile([P, ROWS, P], F32, name="summed")
                summed[u].append(bank)
                nc.tensor.matmul(
                    out=bank[:], lhsT=identity_bf[:],
                    rhs=mean_sb[u // HALVES][:, first : first + ROWS, P * h : P * (h + 1)],
                    start=True, stop=False,
                )
            for h in range(2):
                for j in range(ROWS):
                    nc.tensor.matmul(
                        out=summed[u][h][:, j, :], lhsT=diagonal[u][:, j, :], rhs=centred[u][:, j, P * h : P * (h + 1)],
                        start=False, stop=(j == ROWS - 1),
                    )

        def grouped_half(u):
            if u // HALVES not in grouped:
                grouped[u // HALVES] = work.tile([P, HALVES, PIXELS, ROWS], BF16, name="grouped", align_bytes=64)
            return grouped[u // HALVES][:, u % HALVES, :, :]

        def collect(u):
            for h in range(2):
                nc.scalar.copy(
                    out=grouped_half(u)[:, P * h : P * (h + 1), :], in_=summed[u][h][:].rearrange("p j n -> p n j")
                )

        def regroup(u):
            nc.scalar.copy(
                out=grouped_half(u).rearrange("p (c i) j -> p c j i", i=RUN),
                in_=modulated[u][:].rearrange("p j (c i) -> p c j i", i=RUN),
            )

        def quantise(b):
            nc.vector.quantize_mx(
                out=o_words[b][:].rearrange("p g n -> p (g n)").bitcast(FP8X4),
                scales=o_scales[b][:].rearrange("p g n -> p (g n)"),
                in_=grouped[b][:].rearrange("p g n j -> p (g n j)"),
            )

        def project(u):
            b = u // HALVES
            projected[u] = []
            for pair in range(ROWS // 2):
                bank = psum_y.tile([P, 2, PIXELS], F32, name="bank")
                projected[u].append(bank)
                for side in range(2):
                    columns = slice(P * (2 * pair + side), P * (2 * pair + side + 1))
                    for g in range(HALVES):
                        nc.tensor.matmul_mx(
                            out=bank[:, side, :],
                            lhsT=w_words[:, u % HALVES, g, columns].bitcast(FP8X4),
                            lhsT_scale=w_scales[:, u % HALVES, g, columns],
                            rhs=o_words[b][:, g, :].bitcast(FP8X4),
                            rhs_scale=o_scales[b][:, g, :],
                            start=(g == 0),
                            stop=(g == HALVES - 1),
                        )

        def finish(u):
            result = work.tile([P, ROWS, PIXELS], F32, name="result", bufs=UNITS)
            for pair in range(ROWS // 2):
                last = u == UNITS - 1 and pair == ROWS // 2 - 1
                for side in range(2):
                    j = 2 * pair + side
                    nc.vector.scalar_tensor_tensor(
                        out=result[:, j, :], in0=projected[u][pair][:, side, :],
                        scalar=bias[:, (u % HALVES) * ROWS + j : (u % HALVES) * ROWS + j + 1],
                        in1=row(x_sb, u, j), op0=ALU.add, op1=ALU.add,
                    )
                    if last:
                        nc.sync.dma_start(
                            out=out_dram[u // HALVES][:, u % HALVES, j * PIXELS : (j + 1) * PIXELS], in_=result[:, j, :]
                        )
                if not last:
                    nc.sync.dma_start(
                        out=out_dram[u // HALVES][:, u % HALVES, 2 * pair * PIXELS : 2 * (pair + 1) * PIXELS],
                        in_=result[:, 2 * pair : 2 * (pair + 1), :].rearrange("p j n -> p (j n)"),
                    )

        def scalar_stats(u):
            if scalar_rows(u):
                scalar_total(u)
                scalar_squares(u)
            scalar_deviation(u)

        vector_stats(0)
        scalar_total(1)
        scalar_deviation(0)
        scalar_squares(1)
        scalar_deviation(1)
        for b in range(IMAGES):
            even, odd = HALVES * b, HALVES * b + 1
            centre_times_std(even)
            if b == 3:
                w_quantise(1)
            centre_times_std(odd)
            if b == 3:
                vector_inverse(even)
            if b < 3:
                vector_inverses(b)
                vector_stats(even + HALVES)
            if b == 3:
                collect(4)
            if even in TENSOR_UNITS:
                diagonals(even)
            if b == 1:
                w_quarter(1)
            if b == 2:
                project(0)
                w_quarter(3)
            if b == 3:
                regroup(5)
                project(2)
                project(1)
                project(3)
            if even in TENSOR_UNITS:
                tensor_scale_plus_mean(even)
            if b == 2:
                finish(0)
            if b == 3:
                finish(2)
                vector_inverse(odd)
                finish(1)
                scale_plus_mean(odd)
            if b > 0:
                quantise(b - 1)
            if even not in TENSOR_UNITS:
                scale_plus_mean(even)
            if b < 3:
                scale_plus_mean(odd)
            if b == 1:
                w_quantise(0)
                nc.vector.tensor_copy(out=bias[:], in_=bias_bf[:].rearrange("p g j -> p (g j)"))
            if b < 2:
                scalar_total(odd + HALVES)
                scalar_deviation(even + HALVES)
                scalar_squares(odd + HALVES)
                scalar_deviation(odd + HALVES)
            if b == 2:
                scalar_stats(6)
                scalar_stats(7)
            if b == 1:
                collect(2)
            if even not in TENSOR_UNITS:
                regroup(even)
            if b != 2:
                regroup(odd)
            if b == 3:
                collect(6)
            if b < 2:
                w_quarter(2 * b)
        finish(3)
        project(4)
        finish(4)
        quantise(3)
        for u in (5, 6, 7):
            project(u)
            finish(u)
